import numpy as np
import ml_dtypes


def mxq(x, axis, fmt="e4m3"):
    dtype, down = {"e4m3": (ml_dtypes.float8_e4m3fn, 7), "e5m2": (ml_dtypes.float8_e5m2, 14)}[fmt]
    v = np.moveaxis(np.asarray(x, np.float32).astype(ml_dtypes.bfloat16).astype(np.float64), axis, -1)
    blocks = v.reshape(v.shape[:-1] + (-1, 32))
    amax = np.abs(blocks).max(-1, keepdims=True)
    byte = np.maximum(np.where(amax > 0, np.frexp(amax)[1] - 1 + 127, 0) - down, 1)
    scale = np.exp2(byte - 127.0)
    codes = (blocks / scale).astype(np.float32).astype(dtype).astype(np.float64)
    return np.moveaxis((codes * scale).reshape(v.shape), -1, axis)


WIDE = False


def mx_kscale(k):
    if not WIDE:
        return np.ones(k)
    levels = np.array([10, -10, 5, -5, 0])
    a = np.random.permutation(np.resize(levels, k // 512 * 4)).reshape(k // 512, 4)
    idx = np.arange(k)
    return np.exp2(a[idx // 512, idx % 128 // 32])


BF16 = ml_dtypes.bfloat16


def bf(x):
    return np.asarray(x, np.float32).astype(BF16)


def f64(x):
    return np.asarray(x).astype(np.float64)


S, M, L1, L2, L3, B, NG = 512, 512, 1024, 1024, 1024, 256, 4


def sigmoid(v):
    return 1.0 / (1.0 + np.exp(-v))


def lstm_cell(x, h, c, Wih, Whh, bih, bhh):
    g = (mxq(x, 1, "e4m3") @ mxq(Wih, 1, "e4m3").T) + (mxq(h, 1, "e4m3") @ mxq(Whh, 1, "e4m3").T) + (bih + bhh)
    i, f, gg, o = np.split(g, NG, axis=-1)
    c_new = sigmoid(f) * c + sigmoid(i) * np.tanh(gg)
    h_new = sigmoid(o) * np.tanh(c_new)
    return h_new, c_new


def setup_inputs():
    rn = np.random.standard_normal
    s, t1, t2 = mx_kscale(S), mx_kscale(L1), mx_kscale(L2)
    return {
        "x": bf(rn((B, S)) * s),
        "h1": bf(rn((B, L1)) * t1), "c1": bf(rn((B, L1))),
        "h2": bf(rn((B, L2)) * t2), "c2": bf(rn((B, L2))),
        "Wih1": bf(rn((NG * L1, S)) * 0.7 / np.sqrt(S) / s), "Whh1": bf(rn((NG * L1, L1)) * 0.7 / np.sqrt(L1) / t1),
        "bih1": bf(rn(NG * L1) * 0.3), "bhh1": bf(rn(NG * L1) * 0.3),
        "Wih2": bf(rn((NG * L2, L1)) * 2.0 / np.sqrt(L1)), "Whh2": bf(rn((NG * L2, L2)) * 0.7 / np.sqrt(L2) / t2),
        "bih2": bf(rn(NG * L2) * 0.3), "bhh2": bf(rn(NG * L2) * 0.3),
    }


def reference(x, h1, c1, h2, c2, Wih1, Whh1, bih1, bhh1, Wih2, Whh2, bih2, bhh2):
    y1, nc1 = lstm_cell(f64(x), f64(h1), f64(c1), f64(Wih1), f64(Whh1), f64(bih1), f64(bhh1))
    y2, nc2 = lstm_cell(y1, f64(h2), f64(c2), f64(Wih2), f64(Whh2), f64(bih2), f64(bhh2))
    return y1, nc1, y2, nc2

@@ -1,0 +1,336 @@
+from contextlib import ExitStack
+
+import concourse.mybir as mybir
+from concourse.masks import make_identity
+
+F32 = mybir.dt.float32
+BF16 = mybir.dt.bfloat16
+U32 = mybir.dt.uint32
+U8 = mybir.dt.uint8
+FP8X4 = mybir.dt.float8_e4m3fn_x4
+ACT = mybir.ActivationFunctionType
+ALU = mybir.AluOpType
+
+P = 128
+B = 256
+L = 1024
+FLOPS = 2 * 256 * 4096 * (512 + 1024 + 1024 + 1024)
+
+NR = 32
+NB = 9
+GATE_ORDER = (1, 0, 2, 3)
+FUNC = (ACT.Sigmoid, ACT.Sigmoid, ACT.Tanh, ACT.Sigmoid)
+
+
+def tile_network_pa_kernel(
+    tc, x, h1, c1, h2, c2, Wih1, Whh1, bih1, bhh1, Wih2, Whh2, bih2, bhh2, out_0, out_1, out_2, out_3
+):
+    nc = tc.nc
+    with ExitStack() as ctx:
+        const = ctx.enter_context(tc.tile_pool(name="const", bufs=1))
+        rawp = ctx.enter_context(tc.tile_pool(name="rawp", bufs=NB))
+        grpp = ctx.enter_context(tc.tile_pool(name="grpp", bufs=3))
+        codp = ctx.enter_context(tc.tile_pool(name="codp", bufs=4))
+        work = ctx.enter_context(tc.tile_pool(name="work", bufs=2))
+        psum = ctx.enter_context(tc.psum_pool(name="psum", bufs=2))
+        ctx.enter_context(tc.manual_schedule())
+
+        def wview(w):
+            return w.rearrange("(g u p e) k -> g u p (e k)", g=4, u=4, p=P, e=2)
+
+        wih = (wview(Wih1), wview(Wih2))
+        whh = (wview(Whh1), wview(Whh2))
+
+        def bank(name):
+            return psum.tile([P, 512], F32, name=name, tag="tp", bufs=6)
+
+        ident = const.tile([P, P], F32, name="ident")
+        make_identity(nc, ident[:])
+        btile = const.tile([P, 256], BF16, name="btile")
+        nc.vector.memset(btile[:], 0.0)
+
+        def act_in(ap, k, name):
+            t = const.tile([P, 2, k], BF16, name=name)
+            nc.sync.dma_start(out=t[:], in_=ap.rearrange("(h b) k -> b h k", h=2))
+            return t
+
+        raw = {}
+        grp = {}
+        cod = {}
+        scl = {}
+        tps = {}
+        mxs = {}
+        gts = {}
+
+        def info(r):
+            return r // 16, (r % 16) // 4, GATE_ORDER[r % 4]
+
+        def load_w(r):
+            cell, up, gate = info(r)
+            t = rawp.tile([P, 4096], BF16, name="raw")
+            kih = 1024 if cell == 0 else 2048
+            nc.sync.dma_start(out=t[:, 0:kih], in_=wih[cell][gate, up])
+            nc.sync.dma_start(out=t[:, kih : kih + 2048], in_=whh[cell][gate, up])
+            raw[r] = t
+
+        KP = (
+            ((0, 256, 0), (512, 512, 1), (768, 512, 2)),
+            ((1024, 512, 3), (1280, 512, 4), (0, 512, 5), (256, 512, 6)),
+        )
+
+        x_sb = act_in(x, 512, "x_sb")
+        h1_sb = act_in(h1, 1024, "h1_sb")
+        load_w(0)
+        for v, bv in enumerate((bih1, bhh1, bih2, bhh2)):
+            nc.gpsimd.dma_start(out=btile[16 * v : 16 * v + 16, :], in_=bv.rearrange("(r w) -> r w", w=256))
+        load_w(1)
+        c1_sb = act_in(c1, 1024, "c1_sb")
+        for r in range(2, 6):
+            load_w(r)
+        h2_sb = act_in(h2, 1024, "h2_sb")
+        c2_sb = act_in(c2, 1024, "c2_sb")
+        for r in range(6, NB):
+            load_w(r)
+        c_sb = (c1_sb, c2_sb)
+
+        actc = const.tile([P, 7, B], U32, name="actc", align_bytes=64)
+        acts = const.tile([P, 7, B], U8, name="acts", align_bytes=64)
+        osb = [const.tile([P, 2, L], F32, name="osb%d" % i) for i in range(4)]
+        outs = [o.rearrange("(h b) l -> b h l", h=2) for o in (out_0, out_1, out_2, out_3)]
+
+        def copy_on(eng, out, in_):
+            if eng == "s":
+                nc.scalar.copy(out=out, in_=in_)
+            else:
+                nc.vector.tensor_copy(out=out, in_=in_)
+
+        def act_prep(src, g, eng):
+            words = src[:].bitcast(F32)
+            tp = bank("tpa")
+            for u in range(2):
+                for h in range(2):
+                    nc.tensor.transpose(
+                        out=tp[:, (u * 2 + h) * P : (u * 2 + h + 1) * P],
+                        in_=words[:, h, g * 256 + u * P : g * 256 + (u + 1) * P],
+                        identity=ident[:],
+                    )
+            ag = work.tile([P, 1024], BF16, name="ag", align_bytes=64)
+            copy_on(
+                eng,
+                ag[:].bitcast(F32).rearrange("p (c u) -> p c u", u=2),
+                tp[:].rearrange("p (u c) -> p c u", u=2),
+            )
+            return ag
+
+        def act_quant(ag, slot):
+            nc.vector.quantize_mx(out=actc[:, slot, :].bitcast(FP8X4), scales=acts[:, slot, :], in_=ag)
+
+        def transposes(r):
+            cell = info(r)[0]
+            words = raw[r][:].bitcast(F32)
+            tps[r] = []
+            for w0, we, slot in KP[cell]:
+                tp = bank("tpw")
+                for e in range(2):
+                    for u in range(2):
+                        a = w0 + e * we + u * P
+                        nc.tensor.transpose(
+                            out=tp[:, (e * 2 + u) * P : (e * 2 + u + 1) * P], in_=words[:, a : a + P], identity=ident[:]
+                        )
+                tps[r].append(tp)
+            if r + NB < NR:
+                load_w(r + NB)
+
+        def evac(r, kp, eng):
+            if kp == 0:
+                grp[r] = grpp.tile([P, 4096], BF16, name="grp", align_bytes=64)
+            copy_on(
+                eng,
+                grp[r][:, kp * 1024 : (kp + 1) * 1024].bitcast(F32).rearrange("p (e n u) -> p e n u", e=2, u=2),
+                tps[r][kp][:].rearrange("p (e u n) -> p e n u", e=2, u=2),
+            )
+
+        def quant(r):
+            cell = info(r)[0]
+            cod[r] = codp.tile([P, 1024], U32, name="cod", align_bytes=64)
+            scl[r] = codp.tile([P, 1024], U8, name="scl", align_bytes=64)
+            for a, n in ((0, 2048), (2048, 1024)) if cell == 0 else ((0, 4096),):
+                nc.vector.quantize_mx(
+                    out=cod[r][:, a // 4 : (a + n) // 4].bitcast(FP8X4),
+                    scales=scl[r][:, a // 4 : (a + n) // 4],
+                    in_=grp[r][:, a : a + n],
+                )
+
+        def matmuls(r):
+            cell = info(r)[0]
+            mx = psum.tile([P, 512], F32, name="mx", tag="mx", bufs=2)
+            n = len(KP[cell])
+            for e in range(2):
+                for kp in range(n):
+                    slot = KP[cell][kp][2]
+                    c0 = kp * 256 + e * P
+                    nc.tensor.matmul_mx(
+                        out=mx[:, e * B : (e + 1) * B],
+                        lhsT=cod[r][:, c0 : c0 + P].bitcast(FP8X4),
+                        lhsT_scale=scl[r][:, c0 : c0 + P],
+                        rhs=actc[:, slot, :].bitcast(FP8X4),
+                        rhs_scale=acts[:, slot, :],
+                        start=(kp == 0),
+                        stop=(kp == n - 1),
+                    )
+            mxs[r] = mx
+
+        bsum = const.tile([P, 64], F32, name="bsum")
+
+        def gate_act(r):
+            cell, up, gate = info(r)
+            gt = work.tile([P, 2, B], F32, name="gate%d" % gate)
+            for e in range(2):
+                i = cell * 32 + (gate * 4 + up) * 2 + e
+                nc.scalar.activation(
+                    out=gt[:, e, :], in_=mxs[r][:, e * B : (e + 1) * B], func=FUNC[gate], bias=bsum[:, i : i + 1]
+                )
+            gts[(cell, up, gate)] = gt
+
+        st = {}
+
+        def c_transposes(cell, up):
+            words = c_sb[cell][:].bitcast(F32)
+            tp = bank("tpc")
+            for h in range(2):
+                nc.tensor.transpose(
+                    out=tp[:, h * P : (h + 1) * P], in_=words[:, h, up * P : (up + 1) * P], identity=ident[:]
+                )
+            st[("ct", cell, up)] = tp
+
+        def x_fc(cell, up):
+            t1 = work.tile([P, 2, B], F32, name="t1")
+            ct = st[("ct", cell, up)][:, 0:B].bitcast(BF16).rearrange("p (c e) -> p e c", e=2)
+            nc.vector.tensor_tensor(out=t1[:], in0=gts[(cell, up, 1)][:], in1=ct, op=ALU.mult)
+            st[("t1", cell, up)] = t1
+
+        def x_cn(cell, up):
+            t2 = work.tile([P, 2, B], F32, name="t2")
+            nc.vector.tensor_tensor(out=t2[:], in0=gts[(cell, up, 0)][:], in1=gts[(cell, up, 2)][:], op=ALU.mult)
+            cn = work.tile([P, 2, B], F32, name="cn")
+            nc.vector.tensor_tensor(out=cn[:], in0=st[("t1", cell, up)][:], in1=t2[:], op=ALU.add)
+            st[("cn", cell, up)] = cn
+
+        def x_tanh(cell, up):
+            th = work.tile([P, 2, B], F32, name="th")
+            nc.scalar.activation(out=th[:], in_=st[("cn", cell, up)][:], func=ACT.Tanh)
+            st[("th", cell, up)] = th
+
+        def x_y(cell, up):
+            y = work.tile([P, 2, B], F32, name="y")
+            nc.vector.tensor_tensor(out=y[:], in0=gts[(cell, up, 3)][:], in1=st[("th", cell, up)][:], op=ALU.mult)
+            st[("y", cell, up)] = y
+            if cell == 0:
+                g, u = up // 2, up % 2
+                if u == 0:
+                    st[("ygr", g)] = work.tile([P, B, 4], BF16, name="ygr", align_bytes=64)
+                nc.vector.tensor_copy(
+                    out=st[("ygr", g)][:, :, 2 * u : 2 * u + 2], in_=y[:].rearrange("p e c -> p c e")
+                )
+                if u == 1:
+                    act_quant(st[("ygr", g)][:].rearrange("p c t -> p (c t)"), 5 + g)
+
+        def out_transposes(kind, cell, up):
+            src = st[(kind, cell, up)]
+            tp = bank("tpo")
+            for h in range(2):
+                for e in range(2):
+                    nc.tensor.transpose(
+                        out=tp[:, (h * 2 + e) * P : (h * 2 + e + 1) * P],
+                        in_=src[:, e, h * P : (h + 1) * P],
+                        identity=ident[:],
+                    )
+            st[("o" + kind, cell, up)] = tp
+
+        def out_evac(kind, cell, up, eng):
+            o = cell * 2 + (0 if kind == "y" else 1)
+            copy_on(
+                eng,
+                osb[o][:, :, up * 256 : (up + 1) * 256].rearrange("b h (p e) -> b h p e", e=2),
+                st[("o" + kind, cell, up)][:].rearrange("b (h e p) -> b h p e", h=2, e=2),
+            )
+            lo = -1
+            if cell == 0 and up == 3:
+                lo = 0
+            if cell == 1 and up >= 2:
+                lo = 0 if up == 2 else 768
+            if lo >= 0:
+                hi = (up + 1) * 256
+                nc.sync.dma_start(out=outs[o][:, :, lo:hi], in_=osb[o][:, :, lo:hi])
+
+        warm = const.tile([P, 1], F32, name="warm")
+        nc.vector.memset(warm[:], 0.0)
+        nc.scalar.activation(out=warm[:], in_=warm[:], func=ACT.Sigmoid)
+        ags = [act_prep(x_sb, 0, "s"), act_prep(h1_sb, 0, "v")]
+        act_quant(ags[0][:], 0)
+        ags.append(act_prep(h1_sb, 1, "s"))
+        act_quant(ags[1][:], 1)
+        act_quant(ags[2][:], 2)
+        tpb = bank("tpb")
+        nc.tensor.transpose(out=tpb[:, 0:P], in_=btile[:].bitcast(F32), identity=ident[:])
+        bias_f = const.tile([P, P], F32, name="bias_f")
+        nc.vector.tensor_copy(out=bias_f[:], in_=tpb[:, 0:64].bitcast(BF16))
+        for cell in range(2):
+            nc.vector.tensor_tensor(
+                out=bsum[:, cell * 32 : cell * 32 + 32],
+                in0=bias_f[:, cell * 64 : cell * 64 + 32],
+                in1=bias_f[:, cell * 64 + 32 : cell * 64 + 64],
+                op=ALU.add,
+            )
+
+        t_sched = {}
+        for s in range(-2, 16):
+            t_sched[s] = [s + 2]
+        t_sched[16] = [18, 19]
+        for s in range(17, NR):
+            t_sched[s] = [s + 3] if s + 3 < NR else []
+
+        def evacs(r):
+            n = len(KP[info(r)[0]])
+            for kp in range(n):
+                evac(r, kp, "v" if kp == n - 1 else "s")
+
+        for s in range(-2, NR + 2):
+            rounds = t_sched.get(s, [])
+            j = s % 4
+            blk = s // 4 if s >= 0 else -1
+            pb = blk - 1
+            inside = 0 <= s < NR
+            if rounds:
+                transposes(rounds[0])
+            if inside and j == 2:
+                c_transposes(blk // 4, blk % 4)
+            if s in (9, 11):
+                st[("ag2", s)] = act_prep(h2_sb, (s - 9) // 2, "s")
+            if s >= 4 and j == 0:
+                out_transposes("cn", pb // 4, pb % 4)
+            if s >= 5 and j == 1:
+                out_transposes("y", pb // 4, pb % 4)
+            if 1 <= s <= NR:
+                gate_act(s - 1)
+            for r in t_sched.get(s - 1, []):
+                quant(r)
+            if s in (10, 12):
+                act_quant(st[("ag2", s - 1)][:], 3 + (s - 10) // 2)
+            if rounds:
+                evacs(rounds[0])
+            for r in rounds[1:]:
+                transposes(r)
+                evacs(r)
+            if inside and j == 2:
+                x_fc(blk // 4, blk % 4)
+            if inside and j == 3:
+                x_cn(blk // 4, blk % 4)
+                x_tanh(blk // 4, blk % 4)
+            if s >= 4 and j == 0:
+                x_y(pb // 4, pb % 4)
+                out_evac("cn", pb // 4, pb % 4, "s")
+            if s >= 5 and j == 1:
+                out_evac("y", pb // 4, pb % 4, "s" if pb < 4 else "v")
+            if inside:
+                matmuls(s)

@@ -13,13 +13,16 @@ ALU = mybir.AluOpType
 
 P = 128
 B = 256
-L = 1024
 FLOPS = 2 * 256 * 4096 * (512 + 1024 + 1024 + 1024)
 
 NR = 32
 NB = 9
+LAG1 = 2
+LAG2 = 4
 GATE_ORDER = (1, 0, 2, 3)
 FUNC = (ACT.Sigmoid, ACT.Sigmoid, ACT.Tanh, ACT.Sigmoid)
+RUN = 1
+POOL_BLOCKS = (0, 1, 2, 4, 5, 6)
 
 
 def tile_network_pa_kernel(
@@ -29,8 +32,8 @@ def tile_network_pa_kernel(
     with ExitStack() as ctx:
         const = ctx.enter_context(tc.tile_pool(name="const", bufs=1))
         rawp = ctx.enter_context(tc.tile_pool(name="rawp", bufs=NB))
-        grpp = ctx.enter_context(tc.tile_pool(name="grpp", bufs=3))
-        codp = ctx.enter_context(tc.tile_pool(name="codp", bufs=4))
+        grpp = ctx.enter_context(tc.tile_pool(name="grpp", bufs=4))
+        codp = ctx.enter_context(tc.tile_pool(name="codp", bufs=LAG2 + RUN + 1))
         work = ctx.enter_context(tc.tile_pool(name="work", bufs=2))
         psum = ctx.enter_context(tc.psum_pool(name="psum", bufs=2))
         ctx.enter_context(tc.manual_schedule())
@@ -40,19 +43,10 @@ def tile_network_pa_kernel(
 
         wih = (wview(Wih1), wview(Wih2))
         whh = (wview(Whh1), wview(Whh2))
+        outs = [o.rearrange("(h b) l -> b h l", h=2) for o in (out_0, out_1, out_2, out_3)]
 
         def bank(name):
             return psum.tile([P, 512], F32, name=name, tag="tp", bufs=6)
-
-        ident = const.tile([P, P], F32, name="ident")
-        make_identity(nc, ident[:])
-        btile = const.tile([P, 256], BF16, name="btile")
-        nc.vector.memset(btile[:], 0.0)
-
-        def act_in(ap, k, name):
-            t = const.tile([P, 2, k], BF16, name=name)
-            nc.sync.dma_start(out=t[:], in_=ap.rearrange("(h b) k -> b h k", h=2))
-            return t
 
         raw = {}
         grp = {}
@@ -61,9 +55,15 @@ def tile_network_pa_kernel(
         tps = {}
         mxs = {}
         gts = {}
+        st = {}
 
         def info(r):
             return r // 16, (r % 16) // 4, GATE_ORDER[r % 4]
+
+        def act_in(ap, k, name):
+            t = const.tile([P, 2, k], BF16, name=name)
+            nc.sync.dma_start(out=t[:], in_=ap.rearrange("(h b) k -> b h k", h=2))
+            return t
 
         def load_w(r):
             cell, up, gate = info(r)
@@ -78,25 +78,32 @@ def tile_network_pa_kernel(
             ((1024, 512, 3), (1280, 512, 4), (0, 512, 5), (256, 512, 6)),
         )
 
-        x_sb = act_in(x, 512, "x_sb")
-        h1_sb = act_in(h1, 1024, "h1_sb")
-        load_w(0)
+        ident = const.tile([P, P], F32, name="ident")
+        make_identity(nc, ident[:])
+        btile = const.tile([P, 256], BF16, name="btile")
+        nc.vector.memset(btile[:], 0.0)
         for v, bv in enumerate((bih1, bhh1, bih2, bhh2)):
-            nc.gpsimd.dma_start(out=btile[16 * v : 16 * v + 16, :], in_=bv.rearrange("(r w) -> r w", w=256))
-        load_w(1)
+            nc.scalar.dma_start(out=btile[16 * v : 16 * v + 16, :], in_=bv.rearrange("(r w) -> r w", w=256))
+        warm = const.tile([P, 1], F32, name="warm")
+        nc.vector.memset(warm[:], 0.0)
+        nc.scalar.activation(out=warm[:], in_=warm[:], func=ACT.Sigmoid)
+
+        x_sb = act_in(x, 512, "x_sb")
+        load_w(0)
+        h1_sb = act_in(h1, 1024, "h1_sb")
+        for r in range(1, 4):
+            load_w(r)
         c1_sb = act_in(c1, 1024, "c1_sb")
-        for r in range(2, 6):
+        for r in range(4, NB):
             load_w(r)
         h2_sb = act_in(h2, 1024, "h2_sb")
         c2_sb = act_in(c2, 1024, "c2_sb")
-        for r in range(6, NB):
-            load_w(r)
         c_sb = (c1_sb, c2_sb)
 
         actc = const.tile([P, 7, B], U32, name="actc", align_bytes=64)
         acts = const.tile([P, 7, B], U8, name="acts", align_bytes=64)
-        osb = [const.tile([P, 2, L], F32, name="osb%d" % i) for i in range(4)]
-        outs = [o.rearrange("(h b) l -> b h l", h=2) for o in (out_0, out_1, out_2, out_3)]
+        bias_f = const.tile([P, P], F32, name="bias_f")
+        bsum = const.tile([P, 64], F32, name="bsum")
 
         def copy_on(eng, out, in_):
             if eng == "s":
@@ -125,6 +132,18 @@ def tile_network_pa_kernel(
         def act_quant(ag, slot):
             nc.vector.quantize_mx(out=actc[:, slot, :].bitcast(FP8X4), scales=acts[:, slot, :], in_=ag)
 
+        def bias_prep():
+            tpb = bank("tpb")
+            nc.tensor.transpose(out=tpb[:, 0:P], in_=btile[:].bitcast(F32), identity=ident[:])
+            nc.vector.tensor_copy(out=bias_f[:], in_=tpb[:, 0:64].bitcast(BF16))
+            for cell in range(2):
+                nc.vector.tensor_tensor(
+                    out=bsum[:, cell * 32 : cell * 32 + 32],
+                    in0=bias_f[:, cell * 64 : cell * 64 + 32],
+                    in1=bias_f[:, cell * 64 + 32 : cell * 64 + 64],
+                    op=ALU.add,
+                )
+
         def transposes(r):
             cell = info(r)[0]
             words = raw[r][:].bitcast(F32)
@@ -141,14 +160,16 @@ def tile_network_pa_kernel(
             if r + NB < NR:
                 load_w(r + NB)
 
-        def evac(r, kp, eng):
-            if kp == 0:
-                grp[r] = grpp.tile([P, 4096], BF16, name="grp", align_bytes=64)
-            copy_on(
-                eng,
-                grp[r][:, kp * 1024 : (kp + 1) * 1024].bitcast(F32).rearrange("p (e n u) -> p e n u", e=2, u=2),
-                tps[r][kp][:].rearrange("p (e u n) -> p e n u", e=2, u=2),
-            )
+        def evacs(r):
+            cell = info(r)[0]
+            n = len(KP[cell])
+            grp[r] = grpp.tile([P, 4096], BF16, name="grp", align_bytes=64)
+            for kp in range(n):
+                copy_on(
+                    "v" if kp == n - 1 else "s",
+                    grp[r][:, kp * 1024 : (kp + 1) * 1024].bitcast(F32).rearrange("p (e n u) -> p e n u", e=2, u=2),
+                    tps[r][kp][:].rearrange("p (e u n) -> p e n u", e=2, u=2),
+                )
 
         def quant(r):
             cell = info(r)[0]
@@ -180,8 +201,6 @@ def tile_network_pa_kernel(
                     )
             mxs[r] = mx
 
-        bsum = const.tile([P, 64], F32, name="bsum")
-
         def gate_act(r):
             cell, up, gate = info(r)
             gt = work.tile([P, 2, B], F32, name="gate%d" % gate)
@@ -190,53 +209,57 @@ def tile_network_pa_kernel(
                 nc.scalar.activation(
                     out=gt[:, e, :], in_=mxs[r][:, e * B : (e + 1) * B], func=FUNC[gate], bias=bsum[:, i : i + 1]
                 )
-            gts[(cell, up, gate)] = gt
+            gts[(r // 4, gate)] = gt
 
-        st = {}
+        def ew(blk):
+            return nc.gpsimd if blk in POOL_BLOCKS else nc.vector
 
-        def c_transposes(cell, up):
-            words = c_sb[cell][:].bitcast(F32)
+        def c_transposes(blk):
+            words = c_sb[blk // 4][:].bitcast(F32)
             tp = bank("tpc")
             for h in range(2):
                 nc.tensor.transpose(
-                    out=tp[:, h * P : (h + 1) * P], in_=words[:, h, up * P : (up + 1) * P], identity=ident[:]
+                    out=tp[:, h * P : (h + 1) * P],
+                    in_=words[:, h, (blk % 4) * P : (blk % 4 + 1) * P],
+                    identity=ident[:],
                 )
-            st[("ct", cell, up)] = tp
+            st[("ct", blk)] = tp
 
-        def x_fc(cell, up):
+        def x_fc(blk):
             t1 = work.tile([P, 2, B], F32, name="t1")
-            ct = st[("ct", cell, up)][:, 0:B].bitcast(BF16).rearrange("p (c e) -> p e c", e=2)
-            nc.vector.tensor_tensor(out=t1[:], in0=gts[(cell, up, 1)][:], in1=ct, op=ALU.mult)
-            st[("t1", cell, up)] = t1
+            ct = st[("ct", blk)][:, 0:B].bitcast(BF16).rearrange("p (c e) -> p e c", e=2)
+            nc.vector.tensor_tensor(out=t1[:], in0=gts[(blk, 1)][:], in1=ct, op=ALU.mult)
+            st[("t1", blk)] = t1
 
-        def x_cn(cell, up):
+        def x_cn(blk):
             t2 = work.tile([P, 2, B], F32, name="t2")
-            nc.vector.tensor_tensor(out=t2[:], in0=gts[(cell, up, 0)][:], in1=gts[(cell, up, 2)][:], op=ALU.mult)
+            ew(blk).tensor_tensor(out=t2[:], in0=gts[(blk, 0)][:], in1=gts[(blk, 2)][:], op=ALU.mult)
             cn = work.tile([P, 2, B], F32, name="cn")
-            nc.vector.tensor_tensor(out=cn[:], in0=st[("t1", cell, up)][:], in1=t2[:], op=ALU.add)
-            st[("cn", cell, up)] = cn
+            ew(blk).tensor_tensor(out=cn[:], in0=st[("t1", blk)][:], in1=t2[:], op=ALU.add)
+            st[("cn", blk)] = cn
 
-        def x_tanh(cell, up):
+        def x_tanh(blk):
             th = work.tile([P, 2, B], F32, name="th")
-            nc.scalar.activation(out=th[:], in_=st[("cn", cell, up)][:], func=ACT.Tanh)
-            st[("th", cell, up)] = th
+            nc.scalar.activation(out=th[:], in_=st[("cn", blk)][:], func=ACT.Tanh)
+            st[("th", blk)] = th
 
-        def x_y(cell, up):
+        def x_y(blk):
             y = work.tile([P, 2, B], F32, name="y")
-            nc.vector.tensor_tensor(out=y[:], in0=gts[(cell, up, 3)][:], in1=st[("th", cell, up)][:], op=ALU.mult)
-            st[("y", cell, up)] = y
-            if cell == 0:
-                g, u = up // 2, up % 2
-                if u == 0:
-                    st[("ygr", g)] = work.tile([P, B, 4], BF16, name="ygr", align_bytes=64)
-                nc.vector.tensor_copy(
-                    out=st[("ygr", g)][:, :, 2 * u : 2 * u + 2], in_=y[:].rearrange("p e c -> p c e")
-                )
-                if u == 1:
-                    act_quant(st[("ygr", g)][:].rearrange("p c t -> p (c t)"), 5 + g)
+            ew(blk).tensor_tensor(out=y[:], in0=gts[(blk, 3)][:], in1=st[("th", blk)][:], op=ALU.mult)
+            st[("y", blk)] = y
 
-        def out_transposes(kind, cell, up):
-            src = st[(kind, cell, up)]
+        def y_quant(blk):
+            g, u = blk // 2, blk % 2
+            if u == 0:
+                st[("ygr", g)] = work.tile([P, B, 4], BF16, name="ygr", align_bytes=64)
+            nc.vector.tensor_copy(
+                out=st[("ygr", g)][:, :, 2 * u : 2 * u + 2], in_=st[("y", blk)][:].rearrange("p e c -> p c e")
+            )
+            if u == 1:
+                act_quant(st[("ygr", g)][:].rearrange("p c t -> p (c t)"), 5 + g)
+
+        def out_transposes(kind, blk):
+            src = st[(kind, blk)]
             tp = bank("tpo")
             for h in range(2):
                 for e in range(2):
@@ -245,92 +268,94 @@ def tile_network_pa_kernel(
                         in_=src[:, e, h * P : (h + 1) * P],
                         identity=ident[:],
                     )
-            st[("o" + kind, cell, up)] = tp
+            st[("o" + kind, blk)] = tp
 
-        def out_evac(kind, cell, up, eng):
-            o = cell * 2 + (0 if kind == "y" else 1)
+        def out_evac(kind, blk):
+            o = (blk // 4) * 2 + (0 if kind == "y" else 1)
+            u = blk % 2
+            if u == 0:
+                st[("osb" + kind)] = work.tile([P, 2, 512], F32, name="osb" + kind)
+            osb = st[("osb" + kind)]
             copy_on(
-                eng,
-                osb[o][:, :, up * 256 : (up + 1) * 256].rearrange("b h (p e) -> b h p e", e=2),
-                st[("o" + kind, cell, up)][:].rearrange("b (h e p) -> b h p e", h=2, e=2),
+                "v",
+                osb[:, :, u * 256 : (u + 1) * 256].rearrange("b h (p e) -> b h p e", e=2),
+                st[("o" + kind, blk)][:].rearrange("b (h e p) -> b h p e", h=2, e=2),
             )
-            lo = -1
-            if cell == 0 and up == 3:
-                lo = 0
-            if cell == 1 and up >= 2:
-                lo = 0 if up == 2 else 768
-            if lo >= 0:
-                hi = (up + 1) * 256
-                nc.sync.dma_start(out=outs[o][:, :, lo:hi], in_=osb[o][:, :, lo:hi])
-
-        warm = const.tile([P, 1], F32, name="warm")
-        nc.vector.memset(warm[:], 0.0)
-        nc.scalar.activation(out=warm[:], in_=warm[:], func=ACT.Sigmoid)
-        ags = [act_prep(x_sb, 0, "s"), act_prep(h1_sb, 0, "v")]
-        act_quant(ags[0][:], 0)
-        ags.append(act_prep(h1_sb, 1, "s"))
-        act_quant(ags[1][:], 1)
-        act_quant(ags[2][:], 2)
-        tpb = bank("tpb")
-        nc.tensor.transpose(out=tpb[:, 0:P], in_=btile[:].bitcast(F32), identity=ident[:])
-        bias_f = const.tile([P, P], F32, name="bias_f")
-        nc.vector.tensor_copy(out=bias_f[:], in_=tpb[:, 0:64].bitcast(BF16))
-        for cell in range(2):
-            nc.vector.tensor_tensor(
-                out=bsum[:, cell * 32 : cell * 32 + 32],
-                in0=bias_f[:, cell * 64 : cell * 64 + 32],
-                in1=bias_f[:, cell * 64 + 32 : cell * 64 + 64],
-                op=ALU.add,
-            )
+            lo = u * 256 if blk >= 6 else 0
+            if u == 1 or blk >= 6:
+                c0 = (blk % 4 - u) * 256
+                nc.sync.dma_start(out=outs[o][:, :, c0 + lo : c0 + (u + 1) * 256], in_=osb[:, :, lo : (u + 1) * 256])
 
         t_sched = {}
-        for s in range(-2, 16):
-            t_sched[s] = [s + 2]
-        t_sched[16] = [18, 19]
-        for s in range(17, NR):
-            t_sched[s] = [s + 3] if s + 3 < NR else []
+        for s in range(-LAG1, NR):
+            t_sched[s] = []
+        for r in range(NR):
+            t_sched[r - LAG1 if r < 16 + LAG1 else max(16, r - LAG2)].append(r)
 
-        def evacs(r):
-            n = len(KP[info(r)[0]])
-            for kp in range(n):
-                evac(r, kp, "v" if kp == n - 1 else "s")
-
-        for s in range(-2, NR + 2):
+        pending = []
+        for s in range(-LAG1, NR + RUN + 2):
             rounds = t_sched.get(s, [])
-            j = s % 4
-            blk = s // 4 if s >= 0 else -1
-            pb = blk - 1
-            inside = 0 <= s < NR
+            gr = s - RUN
+            gated = 0 <= gr < NR
+            j = gr % 4
+            blk = gr // 4
+            urgent = blk not in POOL_BLOCKS
+            if s == -2:
+                st["agx"] = act_prep(x_sb, 0, "s")
+            if s == -1:
+                st["agh0"] = act_prep(h1_sb, 0, "s")
+                st["agh1"] = act_prep(h1_sb, 1, "v")
             if rounds:
                 transposes(rounds[0])
-            if inside and j == 2:
-                c_transposes(blk // 4, blk % 4)
+            if s == 0:
+                bias_prep()
+            if gated and j == 1:
+                c_transposes(blk)
             if s in (9, 11):
                 st[("ag2", s)] = act_prep(h2_sb, (s - 9) // 2, "s")
-            if s >= 4 and j == 0:
-                out_transposes("cn", pb // 4, pb % 4)
-            if s >= 5 and j == 1:
-                out_transposes("y", pb // 4, pb % 4)
-            if 1 <= s <= NR:
-                gate_act(s - 1)
+            go = [p for p in pending if p[0] <= s]
+            pending = [p for p in pending if p[0] > s]
+            for p in go:
+                out_transposes(p[1], p[2])
+            if gated:
+                gate_act(gr)
+                if j == 3 and urgent:
+                    x_tanh(blk)
+            if s == -2:
+                act_quant(st["agx"][:], 0)
+            if s == -1:
+                act_quant(st["agh0"][:], 1)
+                act_quant(st["agh1"][:], 2)
             for r in t_sched.get(s - 1, []):
                 quant(r)
             if s in (10, 12):
                 act_quant(st[("ag2", s - 1)][:], 3 + (s - 10) // 2)
+            if gated and j == 2 and urgent:
+                x_cn(blk)
             if rounds:
                 evacs(rounds[0])
+            if gated and j == 3 and urgent:
+                x_y(blk)
+                if blk < 4:
+                    y_quant(blk)
             for r in rounds[1:]:
                 transposes(r)
                 evacs(r)
-            if inside and j == 2:
-                x_fc(blk // 4, blk % 4)
-            if inside and j == 3:
-                x_cn(blk // 4, blk % 4)
-                x_tanh(blk // 4, blk % 4)
-            if s >= 4 and j == 0:
-                x_y(pb // 4, pb % 4)
-                out_evac("cn", pb // 4, pb % 4, "s")
-            if s >= 5 and j == 1:
-                out_evac("y", pb // 4, pb % 4, "s" if pb < 4 else "v")
-            if inside:
-                matmuls(s)
+            for p in go:
+                out_evac(p[1], p[2])
+            if gated and j == 1:
+                x_fc(blk)
+            if gated and j == 2:
+                if not urgent:
+                    x_cn(blk)
+                pending.append((s + 2 if blk < 7 else s + 1, "cn", blk))
+            if gated and j == 3:
+                if not urgent:
+                    x_tanh(blk)
+                    x_y(blk)
+                pending.append((s + 2 if blk < 7 else s + 1, "y", blk))
+            if gated and j == 0 and blk - 1 in POOL_BLOCKS and blk - 1 < 4:
+                y_quant(blk - 1)
+            if 0 <= s < NR and s % RUN == RUN - 1:
+                for r in range(s - RUN + 1, s + 1):
+                    matmuls(r)

@@ -21,8 +21,8 @@ LAG1 = 2
 LAG2 = 4
 GATE_ORDER = (1, 0, 2, 3)
 FUNC = (ACT.Sigmoid, ACT.Sigmoid, ACT.Tanh, ACT.Sigmoid)
-RUN = 1
-POOL_BLOCKS = (0, 1, 2, 4, 5, 6)
+RUN = 2
+POOL_BLOCKS = (0, 1, 2, 4, 5)
 
 
 def tile_network_pa_kernel(
@@ -292,14 +292,17 @@ def tile_network_pa_kernel(
         for r in range(NR):
             t_sched[r - LAG1 if r < 16 + LAG1 else max(16, r - LAG2)].append(r)
 
+        def gstep(r):
+            return r - r % RUN + RUN
+
         pending = []
-        for s in range(-LAG1, NR + RUN + 2):
+        for s in range(-LAG1, NR + RUN + 3):
             rounds = t_sched.get(s, [])
-            gr = s - RUN
-            gated = 0 <= gr < NR
-            j = gr % 4
-            blk = gr // 4
-            urgent = blk not in POOL_BLOCKS
+            g_rounds = [r for r in range(NR) if gstep(r) == s]
+            b_fc = [b for b in range(8) if gstep(4 * b) + 1 == s]
+            b_cn = [b for b in range(8) if gstep(4 * b + 2) == s]
+            b_y = [b for b in range(8) if gstep(4 * b + 3) == s]
+            b_yq = [b for b in range(4) if gstep(4 * b + 3) + 2 == s and b in POOL_BLOCKS]
             if s == -2:
                 st["agx"] = act_prep(x_sb, 0, "s")
             if s == -1:
@@ -309,18 +312,19 @@ def tile_network_pa_kernel(
                 transposes(rounds[0])
             if s == 0:
                 bias_prep()
-            if gated and j == 1:
-                c_transposes(blk)
+            for b in b_fc:
+                c_transposes(b)
             if s in (9, 11):
                 st[("ag2", s)] = act_prep(h2_sb, (s - 9) // 2, "s")
             go = [p for p in pending if p[0] <= s]
             pending = [p for p in pending if p[0] > s]
             for p in go:
                 out_transposes(p[1], p[2])
-            if gated:
-                gate_act(gr)
-                if j == 3 and urgent:
-                    x_tanh(blk)
+            for r in g_rounds:
+                gate_act(r)
+            for b in b_y:
+                if b not in POOL_BLOCKS and b not in b_cn:
+                    x_tanh(b)
             if s == -2:
                 act_quant(st["agx"][:], 0)
             if s == -1:
@@ -330,32 +334,36 @@ def tile_network_pa_kernel(
                 quant(r)
             if s in (10, 12):
                 act_quant(st[("ag2", s - 1)][:], 3 + (s - 10) // 2)
-            if gated and j == 2 and urgent:
-                x_cn(blk)
+            for b in b_cn:
+                if b not in POOL_BLOCKS:
+                    x_cn(b)
             if rounds:
                 evacs(rounds[0])
-            if gated and j == 3 and urgent:
-                x_y(blk)
-                if blk < 4:
-                    y_quant(blk)
+            for b in b_y:
+                if b not in POOL_BLOCKS:
+                    if b in b_cn:
+                        x_tanh(b)
+                    x_y(b)
+                    if b < 4:
+                        y_quant(b)
             for r in rounds[1:]:
                 transposes(r)
                 evacs(r)
             for p in go:
                 out_evac(p[1], p[2])
-            if gated and j == 1:
-                x_fc(blk)
-            if gated and j == 2:
-                if not urgent:
-                    x_cn(blk)
-                pending.append((s + 2 if blk < 7 else s + 1, "cn", blk))
-            if gated and j == 3:
-                if not urgent:
-                    x_tanh(blk)
-                    x_y(blk)
-                pending.append((s + 2 if blk < 7 else s + 1, "y", blk))
-            if gated and j == 0 and blk - 1 in POOL_BLOCKS and blk - 1 < 4:
-                y_quant(blk - 1)
+            for b in b_fc:
+                x_fc(b)
+            for b in b_cn:
+                if b in POOL_BLOCKS:
+                    x_cn(b)
+                pending.append((s + 2 if b < 7 else s + 1, "cn", b))
+            for b in b_y:
+                if b in POOL_BLOCKS:
+                    x_tanh(b)
+                    x_y(b)
+                pending.append((s + 2 if b < 7 else s + 1, "y", b))
+            for b in b_yq:
+                y_quant(b)
             if 0 <= s < NR and s % RUN == RUN - 1:
                 for r in range(s - RUN + 1, s + 1):
                     matmuls(r)

@@ -21,7 +21,10 @@ LAG1 = 2
 LAG2 = 4
 GATE_ORDER = (1, 0, 2, 3)
 FUNC = (ACT.Sigmoid, ACT.Sigmoid, ACT.Tanh, ACT.Sigmoid)
-RUN = 2
+WARM0 = 5
+WARM1 = 4
+WARM2 = 4
+RUN = 1
 POOL_BLOCKS = (0, 1, 2, 4, 5)
 
 
@@ -110,6 +113,15 @@ def tile_network_pa_kernel(
                 nc.scalar.copy(out=out, in_=in_)
             else:
                 nc.vector.tensor_copy(out=out, in_=in_)
+
+        zeros = const.tile([P, 512], BF16, name="zeros")
+        nc.vector.memset(zeros[:], 0.0)
+
+        def idle_matmuls(n):
+            if n > 0:
+                tp = bank("tpd")
+                for i in range(n):
+                    nc.tensor.matmul(out=tp[:], lhsT=zeros[:, 0:P], rhs=zeros[:], start=True, stop=True)
 
         def act_prep(src, g, eng):
             words = src[:].bitcast(F32)
@@ -304,12 +316,15 @@ def tile_network_pa_kernel(
             b_y = [b for b in range(8) if gstep(4 * b + 3) == s]
             b_yq = [b for b in range(4) if gstep(4 * b + 3) + 2 == s and b in POOL_BLOCKS]
             if s == -2:
+                idle_matmuls(WARM0)
                 st["agx"] = act_prep(x_sb, 0, "s")
             if s == -1:
                 st["agh0"] = act_prep(h1_sb, 0, "s")
                 st["agh1"] = act_prep(h1_sb, 1, "v")
             if rounds:
                 transposes(rounds[0])
+            if s < 0:
+                idle_matmuls(WARM1)
             if s == 0:
                 bias_prep()
             for b in b_fc:
@@ -347,6 +362,7 @@ def tile_network_pa_kernel(
                     if b < 4:
                         y_quant(b)
             for r in rounds[1:]:
+                idle_matmuls(WARM2)
                 transposes(r)
                 evacs(r)
             for p in go:

@@ -23,7 +23,6 @@ GATE_ORDER = (1, 0, 2, 3)
 FUNC = (ACT.Sigmoid, ACT.Sigmoid, ACT.Tanh, ACT.Sigmoid)
 WARM0 = 5
 WARM1 = 4
-WARM2 = 4
 RUN = 1
 POOL_BLOCKS = (0, 1, 2, 4, 5)
 
@@ -194,12 +193,17 @@ def tile_network_pa_kernel(
                     in_=grp[r][:, a : a + n],
                 )
 
-        def matmuls(r):
+        def matmuls(r, early=False):
             cell = info(r)[0]
-            mx = psum.tile([P, 512], F32, name="mx", tag="mx", bufs=2)
             n = len(KP[cell])
-            for e in range(2):
-                for kp in range(n):
+            if r not in mxs:
+                mxs[r] = psum.tile([P, 512], F32, name="mx", tag="mx", bufs=2)
+                todo = [(0, kp) for kp in range(n - 1)] if early else [(e, kp) for e in range(2) for kp in range(n)]
+            else:
+                todo = [(0, n - 1)] + [(1, kp) for kp in range(n)]
+            mx = mxs[r]
+            if True:
+                for e, kp in todo:
                     slot = KP[cell][kp][2]
                     c0 = kp * 256 + e * P
                     nc.tensor.matmul_mx(
@@ -211,7 +215,6 @@ def tile_network_pa_kernel(
                         start=(kp == 0),
                         stop=(kp == n - 1),
                     )
-            mxs[r] = mx
 
         def gate_act(r):
             cell, up, gate = info(r)
@@ -245,19 +248,26 @@ def tile_network_pa_kernel(
 
         def x_cn(blk):
             t2 = work.tile([P, 2, B], F32, name="t2")
-            ew(blk).tensor_tensor(out=t2[:], in0=gts[(blk, 0)][:], in1=gts[(blk, 2)][:], op=ALU.mult)
             cn = work.tile([P, 2, B], F32, name="cn")
-            ew(blk).tensor_tensor(out=cn[:], in0=st[("t1", blk)][:], in1=t2[:], op=ALU.add)
+            for e in range(2):
+                ew(blk).tensor_tensor(
+                    out=t2[:, e, :], in0=gts[(blk, 0)][:, e, :], in1=gts[(blk, 2)][:, e, :], op=ALU.mult
+                )
+                ew(blk).tensor_tensor(out=cn[:, e, :], in0=st[("t1", blk)][:, e, :], in1=t2[:, e, :], op=ALU.add)
             st[("cn", blk)] = cn
 
         def x_tanh(blk):
             th = work.tile([P, 2, B], F32, name="th")
-            nc.scalar.activation(out=th[:], in_=st[("cn", blk)][:], func=ACT.Tanh)
+            for e in range(2):
+                nc.scalar.activation(out=th[:, e, :], in_=st[("cn", blk)][:, e, :], func=ACT.Tanh)
             st[("th", blk)] = th
 
         def x_y(blk):
             y = work.tile([P, 2, B], F32, name="y")
-            ew(blk).tensor_tensor(out=y[:], in0=gts[(blk, 3)][:], in1=st[("th", blk)][:], op=ALU.mult)
+            for e in range(2):
+                ew(blk).tensor_tensor(
+                    out=y[:, e, :], in0=gts[(blk, 3)][:, e, :], in1=st[("th", blk)][:, e, :], op=ALU.mult
+                )
             st[("y", blk)] = y
 
         def y_quant(blk):
@@ -273,8 +283,8 @@ def tile_network_pa_kernel(
         def out_transposes(kind, blk):
             src = st[(kind, blk)]
             tp = bank("tpo")
-            for h in range(2):
-                for e in range(2):
+            for e in range(2):
+                for h in range(2):
                     nc.tensor.transpose(
                         out=tp[:, (h * 2 + e) * P : (h * 2 + e + 1) * P],
                         in_=src[:, e, h * P : (h + 1) * P],
@@ -361,8 +371,8 @@ def tile_network_pa_kernel(
                     x_y(b)
                     if b < 4:
                         y_quant(b)
-            for r in rounds[1:]:
-                idle_matmuls(WARM2)
+            for i, r in enumerate(rounds[1:]):
+                matmuls(s + i, early=True)
                 transposes(r)
                 evacs(r)
             for p in go:

@@ -248,26 +248,19 @@ def tile_network_pa_kernel(
 
         def x_cn(blk):
             t2 = work.tile([P, 2, B], F32, name="t2")
+            ew(blk).tensor_tensor(out=t2[:], in0=gts[(blk, 0)][:], in1=gts[(blk, 2)][:], op=ALU.mult)
             cn = work.tile([P, 2, B], F32, name="cn")
-            for e in range(2):
-                ew(blk).tensor_tensor(
-                    out=t2[:, e, :], in0=gts[(blk, 0)][:, e, :], in1=gts[(blk, 2)][:, e, :], op=ALU.mult
-                )
-                ew(blk).tensor_tensor(out=cn[:, e, :], in0=st[("t1", blk)][:, e, :], in1=t2[:, e, :], op=ALU.add)
+            ew(blk).tensor_tensor(out=cn[:], in0=st[("t1", blk)][:], in1=t2[:], op=ALU.add)
             st[("cn", blk)] = cn
 
         def x_tanh(blk):
             th = work.tile([P, 2, B], F32, name="th")
-            for e in range(2):
-                nc.scalar.activation(out=th[:, e, :], in_=st[("cn", blk)][:, e, :], func=ACT.Tanh)
+            nc.scalar.activation(out=th[:], in_=st[("cn", blk)][:], func=ACT.Tanh)
             st[("th", blk)] = th
 
         def x_y(blk):
             y = work.tile([P, 2, B], F32, name="y")
-            for e in range(2):
-                ew(blk).tensor_tensor(
-                    out=y[:, e, :], in0=gts[(blk, 3)][:, e, :], in1=st[("th", blk)][:, e, :], op=ALU.mult
-                )
+            ew(blk).tensor_tensor(out=y[:], in0=gts[(blk, 3)][:], in1=st[("th", blk)][:], op=ALU.mult)
             st[("y", blk)] = y
 
         def y_quant(blk):
@@ -283,8 +276,8 @@ def tile_network_pa_kernel(
         def out_transposes(kind, blk):
             src = st[(kind, blk)]
             tp = bank("tpo")
-            for e in range(2):
-                for h in range(2):
+            for h in range(2):
+                for e in range(2):
                     nc.tensor.transpose(
                         out=tp[:, (h * 2 + e) * P : (h * 2 + e + 1) * P],
                         in_=src[:, e, h * P : (h + 1) * P],

@@ -12,19 +12,23 @@ ACT = mybir.ActivationFunctionType
 ALU = mybir.AluOpType
 
 P = 128
-B = 256
+BATCH = 256
+SLICE = 256
+ROUNDS = 32
+CELL_ROUNDS = 16
 FLOPS = 2 * 256 * 4096 * (512 + 1024 + 1024 + 1024)
 
-NR = 32
-NB = 9
-LAG1 = 2
-LAG2 = 4
 GATE_ORDER = (1, 0, 2, 3)
-FUNC = (ACT.Sigmoid, ACT.Sigmoid, ACT.Tanh, ACT.Sigmoid)
-WARM0 = 5
-WARM1 = 4
-RUN = 1
-POOL_BLOCKS = (0, 1, 2, 4, 5)
+GATE_FUNC = (ACT.Sigmoid, ACT.Sigmoid, ACT.Tanh, ACT.Sigmoid)
+RAW_BUFS = 9
+AHEAD_1 = 2
+AHEAD_2 = 4
+
+K_PASSES = (
+    ((0, 256, 0), (512, 512, 1), (768, 512, 2)),
+    ((1024, 512, 3), (1280, 512, 4), (0, 512, 5), (256, 512, 6)),
+)
+ACT_PASSES = 7
 
 
 def tile_network_pa_kernel(
@@ -33,248 +37,221 @@ def tile_network_pa_kernel(
     nc = tc.nc
     with ExitStack() as ctx:
         const = ctx.enter_context(tc.tile_pool(name="const", bufs=1))
-        rawp = ctx.enter_context(tc.tile_pool(name="rawp", bufs=NB))
+        rawp = ctx.enter_context(tc.tile_pool(name="rawp", bufs=RAW_BUFS))
         grpp = ctx.enter_context(tc.tile_pool(name="grpp", bufs=4))
-        codp = ctx.enter_context(tc.tile_pool(name="codp", bufs=LAG2 + RUN + 1))
+        codp = ctx.enter_context(tc.tile_pool(name="codp", bufs=AHEAD_2 + 2))
         work = ctx.enter_context(tc.tile_pool(name="work", bufs=2))
         psum = ctx.enter_context(tc.psum_pool(name="psum", bufs=2))
         ctx.enter_context(tc.manual_schedule())
 
-        def wview(w):
-            return w.rearrange("(g u p e) k -> g u p (e k)", g=4, u=4, p=P, e=2)
+        def by_round(w):
+            return w.rearrange("(g v p e) k -> g v p (e k)", g=4, v=4, p=P, e=2)
 
-        wih = (wview(Wih1), wview(Wih2))
-        whh = (wview(Whh1), wview(Whh2))
+        wih = (by_round(Wih1), by_round(Wih2))
+        whh = (by_round(Whh1), by_round(Whh2))
         outs = [o.rearrange("(h b) l -> b h l", h=2) for o in (out_0, out_1, out_2, out_3)]
 
         def bank(name):
             return psum.tile([P, 512], F32, name=name, tag="tp", bufs=6)
 
+        def round_of(r):
+            return r // CELL_ROUNDS, (r % CELL_ROUNDS) // 4, GATE_ORDER[r % 4]
+
         raw = {}
-        grp = {}
-        cod = {}
-        scl = {}
-        tps = {}
-        mxs = {}
-        gts = {}
-        st = {}
+        banks = {}
+        grouped = {}
+        words = {}
+        scales = {}
+        sums = {}
+        gates = {}
+        state = {}
 
-        def info(r):
-            return r // 16, (r % 16) // 4, GATE_ORDER[r % 4]
-
-        def act_in(ap, k, name):
+        def load_rows(ap, k, name):
             t = const.tile([P, 2, k], BF16, name=name)
             nc.sync.dma_start(out=t[:], in_=ap.rearrange("(h b) k -> b h k", h=2))
             return t
 
-        def load_w(r):
-            cell, up, gate = info(r)
+        def load_weights(r):
+            cell, sl, gate = round_of(r)
             t = rawp.tile([P, 4096], BF16, name="raw")
-            kih = 1024 if cell == 0 else 2048
-            nc.sync.dma_start(out=t[:, 0:kih], in_=wih[cell][gate, up])
-            nc.sync.dma_start(out=t[:, kih : kih + 2048], in_=whh[cell][gate, up])
+            n_ih = 1024 if cell == 0 else 2048
+            nc.sync.dma_start(out=t[:, 0:n_ih], in_=wih[cell][gate, sl])
+            nc.sync.dma_start(out=t[:, n_ih : n_ih + 2048], in_=whh[cell][gate, sl])
             raw[r] = t
-
-        KP = (
-            ((0, 256, 0), (512, 512, 1), (768, 512, 2)),
-            ((1024, 512, 3), (1280, 512, 4), (0, 512, 5), (256, 512, 6)),
-        )
 
         ident = const.tile([P, P], F32, name="ident")
         make_identity(nc, ident[:])
-        btile = const.tile([P, 256], BF16, name="btile")
-        nc.vector.memset(btile[:], 0.0)
-        for v, bv in enumerate((bih1, bhh1, bih2, bhh2)):
-            nc.scalar.dma_start(out=btile[16 * v : 16 * v + 16, :], in_=bv.rearrange("(r w) -> r w", w=256))
+        bias_rows = const.tile([P, 256], BF16, name="bias_rows")
+        nc.vector.memset(bias_rows[:], 0.0)
+        for v, bias in enumerate((bih1, bhh1, bih2, bhh2)):
+            nc.scalar.dma_start(out=bias_rows[16 * v : 16 * v + 16, :], in_=bias.rearrange("(r w) -> r w", w=256))
         warm = const.tile([P, 1], F32, name="warm")
         nc.vector.memset(warm[:], 0.0)
         nc.scalar.activation(out=warm[:], in_=warm[:], func=ACT.Sigmoid)
 
-        x_sb = act_in(x, 512, "x_sb")
-        load_w(0)
-        h1_sb = act_in(h1, 1024, "h1_sb")
+        x_sb = load_rows(x, 512, "x_sb")
+        load_weights(0)
+        h1_sb = load_rows(h1, 1024, "h1_sb")
         for r in range(1, 4):
-            load_w(r)
-        c1_sb = act_in(c1, 1024, "c1_sb")
-        for r in range(4, NB):
-            load_w(r)
-        h2_sb = act_in(h2, 1024, "h2_sb")
-        c2_sb = act_in(c2, 1024, "c2_sb")
+            load_weights(r)
+        c1_sb = load_rows(c1, 1024, "c1_sb")
+        for r in range(4, RAW_BUFS):
+            load_weights(r)
+        h2_sb = load_rows(h2, 1024, "h2_sb")
+        c2_sb = load_rows(c2, 1024, "c2_sb")
         c_sb = (c1_sb, c2_sb)
 
-        actc = const.tile([P, 7, B], U32, name="actc", align_bytes=64)
-        acts = const.tile([P, 7, B], U8, name="acts", align_bytes=64)
-        bias_f = const.tile([P, P], F32, name="bias_f")
-        bsum = const.tile([P, 64], F32, name="bsum")
+        act_words = const.tile([P, ACT_PASSES, BATCH], U32, name="act_words", align_bytes=64)
+        act_scales = const.tile([P, ACT_PASSES, BATCH], U8, name="act_scales", align_bytes=64)
+        bias_f32 = const.tile([P, P], F32, name="bias_f32")
+        bias_sum = const.tile([P, 64], F32, name="bias_sum")
 
-        def copy_on(eng, out, in_):
-            if eng == "s":
-                nc.scalar.copy(out=out, in_=in_)
-            else:
-                nc.vector.tensor_copy(out=out, in_=in_)
-
-        zeros = const.tile([P, 512], BF16, name="zeros")
-        nc.vector.memset(zeros[:], 0.0)
-
-        def idle_matmuls(n):
-            if n > 0:
-                tp = bank("tpd")
-                for i in range(n):
-                    nc.tensor.matmul(out=tp[:], lhsT=zeros[:, 0:P], rhs=zeros[:], start=True, stop=True)
-
-        def act_prep(src, g, eng):
-            words = src[:].bitcast(F32)
+        def transpose_rows(src, g, copier):
+            src_words = src[:].bitcast(F32)
             tp = bank("tpa")
             for u in range(2):
                 for h in range(2):
                     nc.tensor.transpose(
                         out=tp[:, (u * 2 + h) * P : (u * 2 + h + 1) * P],
-                        in_=words[:, h, g * 256 + u * P : g * 256 + (u + 1) * P],
+                        in_=src_words[:, h, g * 256 + u * P : g * 256 + (u + 1) * P],
                         identity=ident[:],
                     )
-            ag = work.tile([P, 1024], BF16, name="ag", align_bytes=64)
-            copy_on(
-                eng,
-                ag[:].bitcast(F32).rearrange("p (c u) -> p c u", u=2),
-                tp[:].rearrange("p (u c) -> p c u", u=2),
+            t = work.tile([P, 4 * BATCH], BF16, name="act_grouped", align_bytes=64)
+            copier(
+                out=t[:].bitcast(F32).rearrange("p (c u) -> p c u", u=2), in_=tp[:].rearrange("p (u c) -> p c u", u=2)
             )
-            return ag
+            return t[:]
 
-        def act_quant(ag, slot):
-            nc.vector.quantize_mx(out=actc[:, slot, :].bitcast(FP8X4), scales=acts[:, slot, :], in_=ag)
+        def quantise_rows(values, a):
+            nc.vector.quantize_mx(
+                out=act_words[:, a, :].bitcast(FP8X4), scales=act_scales[:, a, :], in_=values
+            )
 
-        def bias_prep():
-            tpb = bank("tpb")
-            nc.tensor.transpose(out=tpb[:, 0:P], in_=btile[:].bitcast(F32), identity=ident[:])
-            nc.vector.tensor_copy(out=bias_f[:], in_=tpb[:, 0:64].bitcast(BF16))
+        def biases():
+            tp = bank("tpb")
+            nc.tensor.transpose(out=tp[:, 0:P], in_=bias_rows[:].bitcast(F32), identity=ident[:])
+            nc.vector.tensor_copy(out=bias_f32[:], in_=tp[:, 0:64].bitcast(BF16))
             for cell in range(2):
                 nc.vector.tensor_tensor(
-                    out=bsum[:, cell * 32 : cell * 32 + 32],
-                    in0=bias_f[:, cell * 64 : cell * 64 + 32],
-                    in1=bias_f[:, cell * 64 + 32 : cell * 64 + 64],
+                    out=bias_sum[:, cell * 32 : cell * 32 + 32],
+                    in0=bias_f32[:, cell * 64 : cell * 64 + 32],
+                    in1=bias_f32[:, cell * 64 + 32 : cell * 64 + 64],
                     op=ALU.add,
                 )
 
-        def transposes(r):
-            cell = info(r)[0]
-            words = raw[r][:].bitcast(F32)
-            tps[r] = []
-            for w0, we, slot in KP[cell]:
+        def transpose_weights(r):
+            raw_words = raw[r][:].bitcast(F32)
+            banks[r] = []
+            for first, e_step, a in K_PASSES[round_of(r)[0]]:
                 tp = bank("tpw")
                 for e in range(2):
                     for u in range(2):
-                        a = w0 + e * we + u * P
+                        w = first + e * e_step + u * P
                         nc.tensor.transpose(
-                            out=tp[:, (e * 2 + u) * P : (e * 2 + u + 1) * P], in_=words[:, a : a + P], identity=ident[:]
+                            out=tp[:, (e * 2 + u) * P : (e * 2 + u + 1) * P],
+                            in_=raw_words[:, w : w + P],
+                            identity=ident[:],
                         )
-                tps[r].append(tp)
-            if r + NB < NR:
-                load_w(r + NB)
+                banks[r].append(tp)
+            if r + RAW_BUFS < ROUNDS:
+                load_weights(r + RAW_BUFS)
 
-        def evacs(r):
-            cell = info(r)[0]
-            n = len(KP[cell])
-            grp[r] = grpp.tile([P, 4096], BF16, name="grp", align_bytes=64)
+        def copy_weights(r):
+            grouped[r] = grpp.tile([P, 4096], BF16, name="grouped", align_bytes=64)
+            n = len(banks[r])
             for kp in range(n):
-                copy_on(
-                    "v" if kp == n - 1 else "s",
-                    grp[r][:, kp * 1024 : (kp + 1) * 1024].bitcast(F32).rearrange("p (e n u) -> p e n u", e=2, u=2),
-                    tps[r][kp][:].rearrange("p (e u n) -> p e n u", e=2, u=2),
+                copier = nc.vector.tensor_copy if kp == n - 1 else nc.scalar.copy
+                copier(
+                    out=grouped[r][:, kp * 1024 : (kp + 1) * 1024]
+                    .bitcast(F32)
+                    .rearrange("p (e n u) -> p e n u", e=2, u=2),
+                    in_=banks[r][kp][:].rearrange("p (e u n) -> p e n u", e=2, u=2),
                 )
 
-        def quant(r):
-            cell = info(r)[0]
-            cod[r] = codp.tile([P, 1024], U32, name="cod", align_bytes=64)
-            scl[r] = codp.tile([P, 1024], U8, name="scl", align_bytes=64)
-            for a, n in ((0, 2048), (2048, 1024)) if cell == 0 else ((0, 4096),):
+        def quantise_weights(r):
+            words[r] = codp.tile([P, 1024], U32, name="words", align_bytes=64)
+            scales[r] = codp.tile([P, 1024], U8, name="scales", align_bytes=64)
+            for a, n in ((0, 2048), (2048, 1024)) if len(banks[r]) == 3 else ((0, 4096),):
                 nc.vector.quantize_mx(
-                    out=cod[r][:, a // 4 : (a + n) // 4].bitcast(FP8X4),
-                    scales=scl[r][:, a // 4 : (a + n) // 4],
-                    in_=grp[r][:, a : a + n],
+                    out=words[r][:, a // 4 : (a + n) // 4].bitcast(FP8X4),
+                    scales=scales[r][:, a // 4 : (a + n) // 4],
+                    in_=grouped[r][:, a : a + n],
                 )
 
-        def matmuls(r, early=False):
-            cell = info(r)[0]
-            n = len(KP[cell])
-            if r not in mxs:
-                mxs[r] = psum.tile([P, 512], F32, name="mx", tag="mx", bufs=2)
-                todo = [(0, kp) for kp in range(n - 1)] if early else [(e, kp) for e in range(2) for kp in range(n)]
-            else:
-                todo = [(0, n - 1)] + [(1, kp) for kp in range(n)]
-            mx = mxs[r]
-            if True:
-                for e, kp in todo:
-                    slot = KP[cell][kp][2]
+        def mx_passes(r):
+            passes = K_PASSES[round_of(r)[0]]
+            sums[r] = psum.tile([P, 2 * BATCH], F32, name="sums", tag="mx", bufs=2)
+            for e in range(2):
+                for kp in range(len(passes)):
+                    a = passes[kp][2]
                     c0 = kp * 256 + e * P
                     nc.tensor.matmul_mx(
-                        out=mx[:, e * B : (e + 1) * B],
-                        lhsT=cod[r][:, c0 : c0 + P].bitcast(FP8X4),
-                        lhsT_scale=scl[r][:, c0 : c0 + P],
-                        rhs=actc[:, slot, :].bitcast(FP8X4),
-                        rhs_scale=acts[:, slot, :],
+                        out=sums[r][:, e * BATCH : (e + 1) * BATCH],
+                        lhsT=words[r][:, c0 : c0 + P].bitcast(FP8X4),
+                        lhsT_scale=scales[r][:, c0 : c0 + P],
+                        rhs=act_words[:, a, :].bitcast(FP8X4),
+                        rhs_scale=act_scales[:, a, :],
                         start=(kp == 0),
-                        stop=(kp == n - 1),
+                        stop=(kp == len(passes) - 1),
                     )
 
-        def gate_act(r):
-            cell, up, gate = info(r)
-            gt = work.tile([P, 2, B], F32, name="gate%d" % gate)
+        def apply_gate(r):
+            cell, sl, gate = round_of(r)
+            t = work.tile([P, 2, BATCH], F32, name="gate%d" % gate)
             for e in range(2):
-                i = cell * 32 + (gate * 4 + up) * 2 + e
+                i = cell * 32 + gate * 8 + sl * 2 + e
                 nc.scalar.activation(
-                    out=gt[:, e, :], in_=mxs[r][:, e * B : (e + 1) * B], func=FUNC[gate], bias=bsum[:, i : i + 1]
+                    out=t[:, e, :],
+                    in_=sums[r][:, e * BATCH : (e + 1) * BATCH],
+                    func=GATE_FUNC[gate],
+                    bias=bias_sum[:, i : i + 1],
                 )
-            gts[(r // 4, gate)] = gt
+            gates[(r // 4, gate)] = t
 
-        def ew(blk):
-            return nc.gpsimd if blk in POOL_BLOCKS else nc.vector
-
-        def c_transposes(blk):
-            words = c_sb[blk // 4][:].bitcast(F32)
+        def transpose_c(sl):
+            c_words = c_sb[sl // 4][:].bitcast(F32)
             tp = bank("tpc")
             for h in range(2):
                 nc.tensor.transpose(
                     out=tp[:, h * P : (h + 1) * P],
-                    in_=words[:, h, (blk % 4) * P : (blk % 4 + 1) * P],
+                    in_=c_words[:, h, (sl % 4) * P : (sl % 4 + 1) * P],
                     identity=ident[:],
                 )
-            st[("ct", blk)] = tp
+            state[("c", sl)] = tp[:, 0:BATCH].bitcast(BF16).rearrange("p (c e) -> p e c", e=2)
 
-        def x_fc(blk):
-            t1 = work.tile([P, 2, B], F32, name="t1")
-            ct = st[("ct", blk)][:, 0:B].bitcast(BF16).rearrange("p (c e) -> p e c", e=2)
-            nc.vector.tensor_tensor(out=t1[:], in0=gts[(blk, 1)][:], in1=ct, op=ALU.mult)
-            st[("t1", blk)] = t1
+        def forget(sl):
+            t = work.tile([P, 2, BATCH], F32, name="fc")
+            nc.vector.tensor_tensor(out=t[:], in0=gates[(sl, 1)][:], in1=state[("c", sl)], op=ALU.mult)
+            state[("fc", sl)] = t
 
-        def x_cn(blk):
-            t2 = work.tile([P, 2, B], F32, name="t2")
-            ew(blk).tensor_tensor(out=t2[:], in0=gts[(blk, 0)][:], in1=gts[(blk, 2)][:], op=ALU.mult)
-            cn = work.tile([P, 2, B], F32, name="cn")
-            ew(blk).tensor_tensor(out=cn[:], in0=st[("t1", blk)][:], in1=t2[:], op=ALU.add)
-            st[("cn", blk)] = cn
+        def new_c(sl):
+            ig = work.tile([P, 2, BATCH], F32, name="ig")
+            nc.vector.tensor_tensor(out=ig[:], in0=gates[(sl, 0)][:], in1=gates[(sl, 2)][:], op=ALU.mult)
+            t = work.tile([P, 2, BATCH], F32, name="new_c")
+            nc.vector.tensor_tensor(out=t[:], in0=state[("fc", sl)][:], in1=ig[:], op=ALU.add)
+            state[("nc", sl)] = t
 
-        def x_tanh(blk):
-            th = work.tile([P, 2, B], F32, name="th")
-            nc.scalar.activation(out=th[:], in_=st[("cn", blk)][:], func=ACT.Tanh)
-            st[("th", blk)] = th
+        def tanh_c(sl):
+            t = work.tile([P, 2, BATCH], F32, name="tanh")
+            nc.scalar.activation(out=t[:], in_=state[("nc", sl)][:], func=ACT.Tanh)
+            state[("tanh", sl)] = t
 
-        def x_y(blk):
-            y = work.tile([P, 2, B], F32, name="y")
-            ew(blk).tensor_tensor(out=y[:], in0=gts[(blk, 3)][:], in1=st[("th", blk)][:], op=ALU.mult)
-            st[("y", blk)] = y
+        def new_y(sl):
+            t = work.tile([P, 2, BATCH], F32, name="y")
+            nc.vector.tensor_tensor(out=t[:], in0=gates[(sl, 3)][:], in1=state[("tanh", sl)][:], op=ALU.mult)
+            state[("y", sl)] = t
 
-        def y_quant(blk):
-            g, u = blk // 2, blk % 2
+        def quantise_y1(sl):
+            g, u = sl // 2, sl % 2
             if u == 0:
-                st[("ygr", g)] = work.tile([P, B, 4], BF16, name="ygr", align_bytes=64)
-            nc.vector.tensor_copy(
-                out=st[("ygr", g)][:, :, 2 * u : 2 * u + 2], in_=st[("y", blk)][:].rearrange("p e c -> p c e")
-            )
+                state[("y1", g)] = work.tile([P, BATCH, 4], BF16, name="y1_grouped", align_bytes=64)
+            t = state[("y1", g)]
+            nc.vector.tensor_copy(out=t[:, :, 2 * u : 2 * u + 2], in_=state[("y", sl)][:].rearrange("p e c -> p c e"))
             if u == 1:
-                act_quant(st[("ygr", g)][:].rearrange("p c t -> p (c t)"), 5 + g)
+                quantise_rows(t[:].rearrange("p c t -> p (c t)"), 5 + g)
 
-        def out_transposes(kind, blk):
-            src = st[(kind, blk)]
+        def transpose_result(kind, sl):
+            src = state[(kind, sl)]
             tp = bank("tpo")
             for h in range(2):
                 for e in range(2):
@@ -283,106 +260,85 @@ def tile_network_pa_kernel(
                         in_=src[:, e, h * P : (h + 1) * P],
                         identity=ident[:],
                     )
-            st[("o" + kind, blk)] = tp
+            state[("T" + kind, sl)] = tp
 
-        def out_evac(kind, blk):
-            o = (blk // 4) * 2 + (0 if kind == "y" else 1)
-            u = blk % 2
+        def store_result(kind, sl):
+            u = sl % 2
             if u == 0:
-                st[("osb" + kind)] = work.tile([P, 2, 512], F32, name="osb" + kind)
-            osb = st[("osb" + kind)]
-            copy_on(
-                "v",
-                osb[:, :, u * 256 : (u + 1) * 256].rearrange("b h (p e) -> b h p e", e=2),
-                st[("o" + kind, blk)][:].rearrange("b (h e p) -> b h p e", h=2, e=2),
+                state["out" + kind] = work.tile([P, 2, 2 * SLICE], F32, name="out" + kind)
+            t = state["out" + kind]
+            copier = nc.scalar.copy if kind == "y" else nc.vector.tensor_copy
+            copier(
+                out=t[:, :, u * SLICE : (u + 1) * SLICE].rearrange("b h (p e) -> b h p e", e=2),
+                in_=state[("T" + kind, sl)][:].rearrange("b (h e p) -> b h p e", h=2, e=2),
             )
-            lo = u * 256 if blk >= 6 else 0
-            if u == 1 or blk >= 6:
-                c0 = (blk % 4 - u) * 256
-                nc.sync.dma_start(out=outs[o][:, :, c0 + lo : c0 + (u + 1) * 256], in_=osb[:, :, lo : (u + 1) * 256])
+            out = outs[(sl // 4) * 2 + (0 if kind == "y" else 1)]
+            c0 = (sl % 4 - u) * SLICE
+            if sl >= 6:
+                nc.sync.dma_start(
+                    out=out[:, :, c0 + u * SLICE : c0 + (u + 1) * SLICE], in_=t[:, :, u * SLICE : (u + 1) * SLICE]
+                )
+            elif u == 1:
+                nc.sync.dma_start(out=out[:, :, c0 : c0 + 2 * SLICE], in_=t[:])
 
-        t_sched = {}
-        for s in range(-LAG1, NR):
-            t_sched[s] = []
-        for r in range(NR):
-            t_sched[r - LAG1 if r < 16 + LAG1 else max(16, r - LAG2)].append(r)
+        def rounds_to_transpose(s):
+            if s < CELL_ROUNDS:
+                return [s + AHEAD_1]
+            if s == CELL_ROUNDS:
+                return list(range(s + AHEAD_1, s + AHEAD_2 + 1))
+            return [s + AHEAD_2] if s + AHEAD_2 < ROUNDS else []
 
-        def gstep(r):
-            return r - r % RUN + RUN
+        due = {}
+        for sl in range(8):
+            wait = 2 if sl < 7 else 1
+            due[4 * sl + 3 + wait] = ("nc", sl)
+            due[4 * sl + 4 + wait] = ("y", sl)
 
-        pending = []
-        for s in range(-LAG1, NR + RUN + 3):
-            rounds = t_sched.get(s, [])
-            g_rounds = [r for r in range(NR) if gstep(r) == s]
-            b_fc = [b for b in range(8) if gstep(4 * b) + 1 == s]
-            b_cn = [b for b in range(8) if gstep(4 * b + 2) == s]
-            b_y = [b for b in range(8) if gstep(4 * b + 3) == s]
-            b_yq = [b for b in range(4) if gstep(4 * b + 3) + 2 == s and b in POOL_BLOCKS]
+        for s in range(-AHEAD_1, ROUNDS + 2):
+            todo = rounds_to_transpose(s)
+            gated = s - 1
+            has_gate = 0 <= gated < ROUNDS
+            j = gated % 4 if has_gate else -1
+            sl = gated // 4
+            rows = []
             if s == -2:
-                idle_matmuls(WARM0)
-                st["agx"] = act_prep(x_sb, 0, "s")
+                rows.append((transpose_rows(x_sb, 0, nc.scalar.copy), 0))
             if s == -1:
-                st["agh0"] = act_prep(h1_sb, 0, "s")
-                st["agh1"] = act_prep(h1_sb, 1, "v")
-            if rounds:
-                transposes(rounds[0])
-            if s < 0:
-                idle_matmuls(WARM1)
+                rows.append((transpose_rows(h1_sb, 0, nc.scalar.copy), 1))
+                rows.append((transpose_rows(h1_sb, 1, nc.vector.tensor_copy), 2))
+            if todo:
+                transpose_weights(todo[0])
             if s == 0:
-                bias_prep()
-            for b in b_fc:
-                c_transposes(b)
-            if s in (9, 11):
-                st[("ag2", s)] = act_prep(h2_sb, (s - 9) // 2, "s")
-            go = [p for p in pending if p[0] <= s]
-            pending = [p for p in pending if p[0] > s]
-            for p in go:
-                out_transposes(p[1], p[2])
-            for r in g_rounds:
-                gate_act(r)
-            for b in b_y:
-                if b not in POOL_BLOCKS and b not in b_cn:
-                    x_tanh(b)
-            if s == -2:
-                act_quant(st["agx"][:], 0)
-            if s == -1:
-                act_quant(st["agh0"][:], 1)
-                act_quant(st["agh1"][:], 2)
-            for r in t_sched.get(s - 1, []):
-                quant(r)
-            if s in (10, 12):
-                act_quant(st[("ag2", s - 1)][:], 3 + (s - 10) // 2)
-            for b in b_cn:
-                if b not in POOL_BLOCKS:
-                    x_cn(b)
-            if rounds:
-                evacs(rounds[0])
-            for b in b_y:
-                if b not in POOL_BLOCKS:
-                    if b in b_cn:
-                        x_tanh(b)
-                    x_y(b)
-                    if b < 4:
-                        y_quant(b)
-            for i, r in enumerate(rounds[1:]):
-                matmuls(s + i, early=True)
-                transposes(r)
-                evacs(r)
-            for p in go:
-                out_evac(p[1], p[2])
-            for b in b_fc:
-                x_fc(b)
-            for b in b_cn:
-                if b in POOL_BLOCKS:
-                    x_cn(b)
-                pending.append((s + 2 if b < 7 else s + 1, "cn", b))
-            for b in b_y:
-                if b in POOL_BLOCKS:
-                    x_tanh(b)
-                    x_y(b)
-                pending.append((s + 2 if b < 7 else s + 1, "y", b))
-            for b in b_yq:
-                y_quant(b)
-            if 0 <= s < NR and s % RUN == RUN - 1:
-                for r in range(s - RUN + 1, s + 1):
-                    matmuls(r)
+                biases()
+            if s in (11, 12):
+                rows.append((transpose_rows(h2_sb, s - 11, nc.scalar.copy), 3 + s - 11))
+            if j == 1:
+                transpose_c(sl)
+            if s in due:
+                transpose_result(due[s][0], due[s][1])
+            if has_gate:
+                apply_gate(gated)
+            if j == 3:
+                tanh_c(sl)
+            if s > -AHEAD_1:
+                for r in rounds_to_transpose(s - 1):
+                    quantise_weights(r)
+            if j == 2:
+                new_c(sl)
+            if todo:
+                copy_weights(todo[0])
+            if j == 3:
+                new_y(sl)
+                if sl < 4:
+                    quantise_y1(sl)
+            for r in todo[1:]:
+                transpose_weights(r)
+                copy_weights(r)
+            if s in due:
+                store_result(due[s][0], due[s][1])
+            if j == 1:
+                forget(sl)
+            for values, a in rows:
+                quantise_rows(values, a)
+            if 0 <= s < ROUNDS:
+                mx_passes(s)

@@ -224,19 +224,27 @@ def tile_network_pa_kernel(
             nc.vector.tensor_tensor(out=t[:], in0=gates[(sl, 1)][:], in1=state[("c", sl)], op=ALU.mult)
             state[("fc", sl)] = t
 
-        def new_c(sl):
+        def input_part(sl):
             ig = work.tile([P, 2, BATCH], F32, name="ig")
             nc.vector.tensor_tensor(out=ig[:], in0=gates[(sl, 0)][:], in1=gates[(sl, 2)][:], op=ALU.mult)
+            state[("ig", sl)] = ig
+
+        def new_c(sl):
+            ig = state[("ig", sl)]
             t = work.tile([P, 2, BATCH], F32, name="new_c")
             nc.vector.tensor_tensor(out=t[:], in0=state[("fc", sl)][:], in1=ig[:], op=ALU.add)
             state[("nc", sl)] = t
 
         def tanh_c(sl):
+            if sl >= 4:
+                return
             t = work.tile([P, 2, BATCH], F32, name="tanh")
             nc.scalar.activation(out=t[:], in_=state[("nc", sl)][:], func=ACT.Tanh)
             state[("tanh", sl)] = t
 
         def new_y(sl):
+            if sl >= 4:
+                return
             t = work.tile([P, 2, BATCH], F32, name="y")
             nc.vector.tensor_tensor(out=t[:], in0=gates[(sl, 3)][:], in1=state[("tanh", sl)][:], op=ALU.mult)
             state[("y", sl)] = t
@@ -251,7 +259,7 @@ def tile_network_pa_kernel(
                 quantise_rows(t[:].rearrange("p c t -> p (c t)"), 5 + g)
 
         def transpose_result(kind, sl):
-            src = state[(kind, sl)]
+            src = gates[(sl, 3)] if (kind == "y" and sl >= 4) else state[(kind, sl)]
             tp = bank("tpo")
             for h in range(2):
                 for e in range(2):
@@ -267,11 +275,23 @@ def tile_network_pa_kernel(
             if u == 0:
                 state["out" + kind] = work.tile([P, 2, 2 * SLICE], F32, name="out" + kind)
             t = state["out" + kind]
-            copier = nc.scalar.copy if kind == "y" else nc.vector.tensor_copy
-            copier(
-                out=t[:, :, u * SLICE : (u + 1) * SLICE].rearrange("b h (p e) -> b h p e", e=2),
-                in_=state[("T" + kind, sl)][:].rearrange("b (h e p) -> b h p e", h=2, e=2),
-            )
+            out_view = t[:, :, u * SLICE : (u + 1) * SLICE].rearrange("b h (p e) -> b h p e", e=2)
+            in_view = state[("T" + kind, sl)][:].rearrange("b (h e p) -> b h p e", h=2, e=2)
+            if sl < 4:
+                copier = nc.scalar.copy if kind == "y" else nc.vector.tensor_copy
+                copier(out=out_view, in_=in_view)
+            elif kind == "nc":
+                nc.vector.tensor_copy(out=out_view, in_=in_view)
+                tt = work.tile([P, 512], F32, name="tanh_t")
+                nc.scalar.activation(out=tt[:], in_=state[("T" + kind, sl)][:], func=ACT.Tanh)
+                state[("tanh_t", sl)] = tt
+            else:
+                nc.vector.tensor_tensor(
+                    out=out_view,
+                    in0=in_view,
+                    in1=state[("tanh_t", sl)][:].rearrange("b (h e p) -> b h p e", h=2, e=2),
+                    op=ALU.mult,
+                )
             out = outs[(sl // 4) * 2 + (0 if kind == "y" else 1)]
             c0 = (sl % 4 - u) * SLICE
             if sl >= 6:
@@ -302,14 +322,13 @@ def tile_network_pa_kernel(
             sl = gated // 4
             rows = []
             if s == -2:
+                biases()
                 rows.append((transpose_rows(x_sb, 0, nc.scalar.copy), 0))
             if s == -1:
                 rows.append((transpose_rows(h1_sb, 0, nc.scalar.copy), 1))
                 rows.append((transpose_rows(h1_sb, 1, nc.vector.tensor_copy), 2))
             if todo:
                 transpose_weights(todo[0])
-            if s == 0:
-                biases()
             if s in (11, 12):
                 rows.append((transpose_rows(h2_sb, s - 11, nc.scalar.copy), 3 + s - 11))
             if j == 1:
@@ -324,9 +343,11 @@ def tile_network_pa_kernel(
                 for r in rounds_to_transpose(s - 1):
                     quantise_weights(r)
             if j == 2:
-                new_c(sl)
+                input_part(sl)
             if todo:
                 copy_weights(todo[0])
+            if j == 2:
+                new_c(sl)
             if j == 3:
                 new_y(sl)
                 if sl < 4:

@@ -94,12 +94,12 @@ def tile_network_pa_kernel(
         h1_sb = load_rows(h1, 1024, "h1_sb")
         for r in range(1, 4):
             load_weights(r)
-        c1_sb = load_rows(c1, 1024, "c1_sb")
-        for r in range(4, RAW_BUFS):
+        for r in range(4, 6):
             load_weights(r)
-        h2_sb = load_rows(h2, 1024, "h2_sb")
-        c2_sb = load_rows(c2, 1024, "c2_sb")
-        c_sb = (c1_sb, c2_sb)
+        c1_sb = load_rows(c1, 1024, "c1_sb")
+        for r in range(6, RAW_BUFS):
+            load_weights(r)
+        c_sb = [c1_sb, None]
 
         act_words = const.tile([P, ACT_PASSES, BATCH], U32, name="act_words", align_bytes=64)
         act_scales = const.tile([P, ACT_PASSES, BATCH], U8, name="act_scales", align_bytes=64)
@@ -224,15 +224,24 @@ def tile_network_pa_kernel(
             nc.vector.tensor_tensor(out=t[:], in0=gates[(sl, 1)][:], in1=state[("c", sl)], op=ALU.mult)
             state[("fc", sl)] = t
 
+        def parts(sl):
+            return (slice(0, 1), slice(1, 2)) if sl == 7 else (slice(0, 2),)
+
         def input_part(sl):
             ig = work.tile([P, 2, BATCH], F32, name="ig")
-            nc.vector.tensor_tensor(out=ig[:], in0=gates[(sl, 0)][:], in1=gates[(sl, 2)][:], op=ALU.mult)
+            for part in parts(sl):
+                nc.vector.tensor_tensor(
+                    out=ig[:, part], in0=gates[(sl, 0)][:, part], in1=gates[(sl, 2)][:, part], op=ALU.mult
+                )
             state[("ig", sl)] = ig
 
         def new_c(sl):
             ig = state[("ig", sl)]
             t = work.tile([P, 2, BATCH], F32, name="new_c")
-            nc.vector.tensor_tensor(out=t[:], in0=state[("fc", sl)][:], in1=ig[:], op=ALU.add)
+            for part in parts(sl):
+                nc.vector.tensor_tensor(
+                    out=t[:, part], in0=state[("fc", sl)][:, part], in1=ig[:, part], op=ALU.add
+                )
             state[("nc", sl)] = t
 
         def tanh_c(sl):
@@ -315,6 +324,10 @@ def tile_network_pa_kernel(
             due[4 * sl + 4 + wait] = ("y", sl)
 
         for s in range(-AHEAD_1, ROUNDS + 2):
+            if s == 3:
+                h2_sb = load_rows(h2, 1024, "h2_sb")
+            if s == 10:
+                c_sb[1] = load_rows(c2, 1024, "c2_sb")
             todo = rounds_to_transpose(s)
             gated = s - 1
             has_gate = 0 <= gated < ROUNDS
@@ -322,16 +335,21 @@ def tile_network_pa_kernel(
             sl = gated // 4
             rows = []
             if s == -2:
-                biases()
                 rows.append((transpose_rows(x_sb, 0, nc.scalar.copy), 0))
             if s == -1:
-                rows.append((transpose_rows(h1_sb, 0, nc.scalar.copy), 1))
-                rows.append((transpose_rows(h1_sb, 1, nc.vector.tensor_copy), 2))
+                quantise_weights(0)
+                values = [transpose_rows(h1_sb, 0, nc.scalar.copy), transpose_rows(h1_sb, 1, nc.vector.tensor_copy)]
+                quantise_rows(values[0], 1)
+                quantise_rows(values[1], 2)
+            if 0 <= s < 1:
+                mx_passes(s)
             if todo:
                 transpose_weights(todo[0])
+            if s == -2:
+                biases()
             if s in (11, 12):
                 rows.append((transpose_rows(h2_sb, s - 11, nc.scalar.copy), 3 + s - 11))
-            if j == 1:
+            if (j == 2 if sl == 0 else j == 1):
                 transpose_c(sl)
             if s in due:
                 transpose_result(due[s][0], due[s][1])
@@ -339,14 +357,14 @@ def tile_network_pa_kernel(
                 apply_gate(gated)
             if j == 3:
                 tanh_c(sl)
-            if s > -AHEAD_1:
+            if s > 1 - AHEAD_1:
                 for r in rounds_to_transpose(s - 1):
                     quantise_weights(r)
             if j == 2:
                 input_part(sl)
             if todo:
                 copy_weights(todo[0])
-            if j == 2:
+            if j == 2 and sl > 0:
                 new_c(sl)
             if j == 3:
                 new_y(sl)
@@ -357,9 +375,11 @@ def tile_network_pa_kernel(
                 copy_weights(r)
             if s in due:
                 store_result(due[s][0], due[s][1])
-            if j == 1:
+            if (j == 2 if sl == 0 else j == 1):
                 forget(sl)
+            if j == 2 and sl == 0:
+                new_c(sl)
             for values, a in rows:
                 quantise_rows(values, a)
-            if 0 <= s < ROUNDS:
+            if 1 <= s < ROUNDS:
                 mx_passes(s)

@@ -269,45 +269,54 @@ def tile_network_pa_kernel(
 
         def transpose_result(kind, sl):
             src = gates[(sl, 3)] if (kind == "y" and sl >= 4) else state[(kind, sl)]
-            tp = bank("tpo")
-            for h in range(2):
-                for e in range(2):
-                    nc.tensor.transpose(
-                        out=tp[:, (h * 2 + e) * P : (h * 2 + e + 1) * P],
-                        in_=src[:, e, h * P : (h + 1) * P],
-                        identity=ident[:],
-                    )
-            state[("T" + kind, sl)] = tp
+            for part in batch_parts(sl):
+                tp = bank("tpo")
+                for h in part:
+                    for e in range(2):
+                        nc.tensor.transpose(
+                            out=tp[:, (h * 2 + e) * P : (h * 2 + e + 1) * P],
+                            in_=src[:, e, h * P : (h + 1) * P],
+                            identity=ident[:],
+                        )
+                state[("T" + kind, sl, part[0])] = tp
+
+        def batch_parts(sl):
+            return ((0,), (1,)) if sl == 7 else ((0, 1),)
 
         def store_result(kind, sl):
             u = sl % 2
             if u == 0:
                 state["out" + kind] = work.tile([P, 2, 2 * SLICE], F32, name="out" + kind)
             t = state["out" + kind]
-            out_view = t[:, :, u * SLICE : (u + 1) * SLICE].rearrange("b h (p e) -> b h p e", e=2)
-            in_view = state[("T" + kind, sl)][:].rearrange("b (h e p) -> b h p e", h=2, e=2)
-            if sl < 4:
-                copier = nc.scalar.copy if kind == "y" else nc.vector.tensor_copy
-                copier(out=out_view, in_=in_view)
-            elif kind == "nc":
-                nc.vector.tensor_copy(out=out_view, in_=in_view)
-                tt = work.tile([P, 512], F32, name="tanh_t")
-                nc.scalar.activation(out=tt[:], in_=state[("T" + kind, sl)][:], func=ACT.Tanh)
-                state[("tanh_t", sl)] = tt
-            else:
-                nc.vector.tensor_tensor(
-                    out=out_view,
-                    in0=in_view,
-                    in1=state[("tanh_t", sl)][:].rearrange("b (h e p) -> b h p e", h=2, e=2),
-                    op=ALU.mult,
-                )
             out = outs[(sl // 4) * 2 + (0 if kind == "y" else 1)]
             c0 = (sl % 4 - u) * SLICE
-            if sl >= 6:
-                nc.sync.dma_start(
-                    out=out[:, :, c0 + u * SLICE : c0 + (u + 1) * SLICE], in_=t[:, :, u * SLICE : (u + 1) * SLICE]
-                )
-            elif u == 1:
+            if kind == "nc" and sl >= 4:
+                state[("tanh_t", sl)] = work.tile([P, 512], F32, name="tanh_t")
+            for part in batch_parts(sl):
+                hs = slice(part[0], part[-1] + 1)
+                cols = slice(part[0] * 256, (part[-1] + 1) * 256)
+                tp = state[("T" + kind, sl, part[0])][:, cols]
+                n = len(part)
+                out_view = t[:, hs, u * SLICE : (u + 1) * SLICE].rearrange("b h (p e) -> b h p e", e=2)
+                in_view = tp.rearrange("b (h e p) -> b h p e", h=n, e=2)
+                if sl < 4:
+                    copier = nc.scalar.copy if kind == "y" else nc.vector.tensor_copy
+                    copier(out=out_view, in_=in_view)
+                elif kind == "nc":
+                    nc.scalar.activation(out=state[("tanh_t", sl)][:, cols], in_=tp, func=ACT.Tanh)
+                    nc.vector.tensor_copy(out=out_view, in_=in_view)
+                else:
+                    nc.vector.tensor_tensor(
+                        out=out_view,
+                        in0=in_view,
+                        in1=state[("tanh_t", sl)][:, cols].rearrange("b (h e p) -> b h p e", h=n, e=2),
+                        op=ALU.mult,
+                    )
+                if sl >= 6:
+                    nc.sync.dma_start(
+                        out=out[:, hs, c0 + u * SLICE : c0 + (u + 1) * SLICE], in_=t[:, hs, u * SLICE : (u + 1) * SLICE]
+                    )
+            if sl < 6 and u == 1:
                 nc.sync.dma_start(out=out[:, :, c0 : c0 + 2 * SLICE], in_=t[:])
 
         def rounds_to_transpose(s):
@@ -337,12 +346,8 @@ def tile_network_pa_kernel(
             if s == -2:
                 rows.append((transpose_rows(x_sb, 0, nc.scalar.copy), 0))
             if s == -1:
-                quantise_weights(0)
-                values = [transpose_rows(h1_sb, 0, nc.scalar.copy), transpose_rows(h1_sb, 1, nc.vector.tensor_copy)]
-                quantise_rows(values[0], 1)
-                quantise_rows(values[1], 2)
-            if 0 <= s < 1:
-                mx_passes(s)
+                rows.append((transpose_rows(h1_sb, 0, nc.scalar.copy), 1))
+                rows.append((transpose_rows(h1_sb, 1, nc.vector.tensor_copy), 2))
             if todo:
                 transpose_weights(todo[0])
             if s == -2:
@@ -357,7 +362,7 @@ def tile_network_pa_kernel(
                 apply_gate(gated)
             if j == 3:
                 tanh_c(sl)
-            if s > 1 - AHEAD_1:
+            if s > -AHEAD_1:
                 for r in rounds_to_transpose(s - 1):
                     quantise_weights(r)
             if j == 2:
@@ -381,5 +386,5 @@ def tile_network_pa_kernel(
                 new_c(sl)
             for values, a in rows:
                 quantise_rows(values, a)
-            if 1 <= s < ROUNDS:
+            if 0 <= s < ROUNDS:
                 mx_passes(s)

@@ -106,7 +106,7 @@ def tile_network_pa_kernel(
         bias_f32 = const.tile([P, P], F32, name="bias_f32")
         bias_sum = const.tile([P, 64], F32, name="bias_sum")
 
-        def transpose_rows(src, g, copier):
+        def transpose_rows(src, g):
             src_words = src[:].bitcast(F32)
             tp = bank("tpa")
             for u in range(2):
@@ -116,6 +116,9 @@ def tile_network_pa_kernel(
                         in_=src_words[:, h, g * 256 + u * P : g * 256 + (u + 1) * P],
                         identity=ident[:],
                     )
+            return tp
+
+        def copy_rows(tp, copier):
             t = work.tile([P, 4 * BATCH], BF16, name="act_grouped", align_bytes=64)
             copier(
                 out=t[:].bitcast(F32).rearrange("p (c u) -> p c u", u=2), in_=tp[:].rearrange("p (u c) -> p c u", u=2)
@@ -160,7 +163,7 @@ def tile_network_pa_kernel(
             grouped[r] = grpp.tile([P, 4096], BF16, name="grouped", align_bytes=64)
             n = len(banks[r])
             for kp in range(n):
-                copier = nc.vector.tensor_copy if kp == n - 1 else nc.scalar.copy
+                copier = nc.vector.tensor_copy if kp == n - 1 and (r >= 16 or r % 2 != 1) else nc.scalar.copy
                 copier(
                     out=grouped[r][:, kp * 1024 : (kp + 1) * 1024]
                     .bitcast(F32)
@@ -344,16 +347,16 @@ def tile_network_pa_kernel(
             sl = gated // 4
             rows = []
             if s == -2:
-                rows.append((transpose_rows(x_sb, 0, nc.scalar.copy), 0))
+                rows.append((copy_rows(transpose_rows(x_sb, 0), nc.scalar.copy), 0))
             if s == -1:
-                rows.append((transpose_rows(h1_sb, 0, nc.scalar.copy), 1))
-                rows.append((transpose_rows(h1_sb, 1, nc.vector.tensor_copy), 2))
+                rows.append((copy_rows(transpose_rows(h1_sb, 0), nc.scalar.copy), 1))
+                rows.append((copy_rows(transpose_rows(h1_sb, 1), nc.vector.tensor_copy), 2))
             if todo:
                 transpose_weights(todo[0])
             if s == -2:
                 biases()
             if s in (11, 12):
-                rows.append((transpose_rows(h2_sb, s - 11, nc.scalar.copy), 3 + s - 11))
+                h2_bank = transpose_rows(h2_sb, s - 11)
             if (j == 2 if sl == 0 else j == 1):
                 transpose_c(sl)
             if s in due:
@@ -384,6 +387,8 @@ def tile_network_pa_kernel(
                 forget(sl)
             if j == 2 and sl == 0:
                 new_c(sl)
+            if s in (11, 12):
+                rows.append((copy_rows(h2_bank, nc.scalar.copy), 3 + s - 11))
             for values, a in rows:
                 quantise_rows(values, a)
             if 0 <= s < ROUNDS:

@@ -22,7 +22,7 @@ GATE_ORDER = (1, 0, 2, 3)
 GATE_FUNC = (ACT.Sigmoid, ACT.Sigmoid, ACT.Tanh, ACT.Sigmoid)
 RAW_BUFS = 9
 AHEAD_1 = 2
-AHEAD_2 = 4
+AHEAD_2 = 3
 
 K_PASSES = (
     ((0, 256, 0), (512, 512, 1), (768, 512, 2)),
@@ -181,15 +181,18 @@ def tile_network_pa_kernel(
                     in_=grouped[r][:, a : a + n],
                 )
 
-        def mx_passes(r):
+        def mx_passes(r, kps=None):
             passes = K_PASSES[round_of(r)[0]]
-            sums[r] = psum.tile([P, 2 * BATCH], F32, name="sums", tag="mx", bufs=2)
+            if kps is None or 0 in kps:
+                sums[r] = [psum.tile([P, 2 * BATCH], F32, name="sums", tag="mx", bufs=2)]
+                if kps is not None:
+                    sums[r].append(psum.tile([P, 2 * BATCH], F32, name="sums", tag="mx", bufs=2))
             for e in range(2):
-                for kp in range(len(passes)):
+                for kp in kps or range(len(passes)):
                     a = passes[kp][2]
                     c0 = kp * 256 + e * P
                     nc.tensor.matmul_mx(
-                        out=sums[r][:, e * BATCH : (e + 1) * BATCH],
+                        out=sum_of(r, e),
                         lhsT=words[r][:, c0 : c0 + P].bitcast(FP8X4),
                         lhsT_scale=scales[r][:, c0 : c0 + P],
                         rhs=act_words[:, a, :].bitcast(FP8X4),
@@ -198,6 +201,11 @@ def tile_network_pa_kernel(
                         stop=(kp == len(passes) - 1),
                     )
 
+        def sum_of(r, e):
+            if len(sums[r]) == 2:
+                return sums[r][e][:, 0:BATCH]
+            return sums[r][0][:, e * BATCH : (e + 1) * BATCH]
+
         def apply_gate(r):
             cell, sl, gate = round_of(r)
             t = work.tile([P, 2, BATCH], F32, name="gate%d" % gate)
@@ -205,7 +213,7 @@ def tile_network_pa_kernel(
                 i = cell * 32 + gate * 8 + sl * 2 + e
                 nc.scalar.activation(
                     out=t[:, e, :],
-                    in_=sums[r][:, e * BATCH : (e + 1) * BATCH],
+                    in_=sum_of(r, e),
                     func=GATE_FUNC[gate],
                     bias=bias_sum[:, i : i + 1],
                 )
@@ -378,6 +386,8 @@ def tile_network_pa_kernel(
                 new_y(sl)
                 if sl < 4:
                     quantise_y1(sl)
+            if s == CELL_ROUNDS:
+                mx_passes(s, range(3))
             for r in todo[1:]:
                 transpose_weights(r)
                 copy_weights(r)
@@ -392,4 +402,4 @@ def tile_network_pa_kernel(
             for values, a in rows:
                 quantise_rows(values, a)
             if 0 <= s < ROUNDS:
-                mx_passes(s)
+                mx_passes(s, range(3, 4) if s == CELL_ROUNDS else None)

@@ -89,6 +89,14 @@ def tile_network_pa_kernel(
         nc.vector.memset(warm[:], 0.0)
         nc.scalar.activation(out=warm[:], in_=warm[:], func=ACT.Sigmoid)
 
+        zeros = const.tile([P, 512], BF16, name="zeros")
+        nc.vector.memset(zeros[:], 0.0)
+
+        def fill(n):
+            for i in range(n):
+                t = psum.tile([P, 2 * BATCH], F32, name="fill", tag="mx", bufs=2)
+                nc.tensor.matmul(out=t[:], lhsT=zeros[:, 0:P], rhs=zeros[:], start=True, stop=True)
+
         x_sb = load_rows(x, 512, "x_sb")
         load_weights(0)
         h1_sb = load_rows(h1, 1024, "h1_sb")
@@ -184,9 +192,12 @@ def tile_network_pa_kernel(
         def mx_passes(r, kps=None):
             passes = K_PASSES[round_of(r)[0]]
             if kps is None or 0 in kps:
-                sums[r] = [psum.tile([P, 2 * BATCH], F32, name="sums", tag="mx", bufs=2)]
-                if kps is not None:
-                    sums[r].append(psum.tile([P, 2 * BATCH], F32, name="sums", tag="mx", bufs=2))
+                if r >= 30:
+                    sums[r] = [bank("sums"), bank("sums")]
+                else:
+                    sums[r] = [psum.tile([P, 2 * BATCH], F32, name="sums", tag="mx", bufs=2)]
+                    if kps is not None:
+                        sums[r].append(psum.tile([P, 2 * BATCH], F32, name="sums", tag="mx", bufs=2))
             for e in range(2):
                 for kp in kps or range(len(passes)):
                     a = passes[kp][2]
@@ -330,6 +341,7 @@ def tile_network_pa_kernel(
             if sl < 6 and u == 1:
                 nc.sync.dma_start(out=out[:, :, c0 : c0 + 2 * SLICE], in_=t[:])
 
+        fill(6)
         def rounds_to_transpose(s):
             if s < CELL_ROUNDS:
                 return [s + AHEAD_1]
@@ -361,6 +373,8 @@ def tile_network_pa_kernel(
                 rows.append((copy_rows(transpose_rows(h1_sb, 1), nc.vector.tensor_copy), 2))
             if todo:
                 transpose_weights(todo[0])
+            if s < 0:
+                fill(2)
             if s == -2:
                 biases()
             if s in (11, 12):

@@ -73,13 +73,13 @@ def tile_network_pa_kernel(
 
         def load_weights(r):
             cell, sl, gate = round_of(r)
-            t = rawp.tile([P, 4096], BF16, name="raw")
+            t = rawp.tile([P, 4096], BF16, name="raw", align_bytes=256)
             n_ih = 1024 if cell == 0 else 2048
             nc.sync.dma_start(out=t[:, 0:n_ih], in_=wih[cell][gate, sl])
             nc.sync.dma_start(out=t[:, n_ih : n_ih + 2048], in_=whh[cell][gate, sl])
             raw[r] = t
 
-        ident = const.tile([P, P], F32, name="ident")
+        ident = const.tile([P, P], F32, name="ident", align_bytes=256)
         make_identity(nc, ident[:])
         bias_rows = const.tile([P, 256], BF16, name="bias_rows")
         nc.vector.memset(bias_rows[:], 0.0)
@@ -109,8 +109,8 @@ def tile_network_pa_kernel(
             load_weights(r)
         c_sb = [c1_sb, None]
 
-        act_words = const.tile([P, ACT_PASSES, BATCH], U32, name="act_words", align_bytes=64)
-        act_scales = const.tile([P, ACT_PASSES, BATCH], U8, name="act_scales", align_bytes=64)
+        act_words = const.tile([P, ACT_PASSES, BATCH], U32, name="act_words", align_bytes=256)
+        act_scales = const.tile([P, ACT_PASSES, BATCH], U8, name="act_scales", align_bytes=256)
         bias_f32 = const.tile([P, P], F32, name="bias_f32")
         bias_sum = const.tile([P, 64], F32, name="bias_sum")
 
@@ -127,7 +127,7 @@ def tile_network_pa_kernel(
             return tp
 
         def copy_rows(tp, copier):
-            t = work.tile([P, 4 * BATCH], BF16, name="act_grouped", align_bytes=64)
+            t = work.tile([P, 4 * BATCH], BF16, name="act_grouped", align_bytes=256)
             copier(
                 out=t[:].bitcast(F32).rearrange("p (c u) -> p c u", u=2), in_=tp[:].rearrange("p (u c) -> p c u", u=2)
             )
@@ -168,7 +168,7 @@ def tile_network_pa_kernel(
                 load_weights(r + RAW_BUFS)
 
         def copy_weights(r):
-            grouped[r] = grpp.tile([P, 4096], BF16, name="grouped", align_bytes=64)
+            grouped[r] = grpp.tile([P, 4096], BF16, name="grouped", align_bytes=256)
             n = len(banks[r])
             for kp in range(n):
                 copier = nc.vector.tensor_copy if kp == n - 1 and (r >= 16 or r % 2 != 1) else nc.scalar.copy
@@ -180,8 +180,8 @@ def tile_network_pa_kernel(
                 )
 
         def quantise_weights(r):
-            words[r] = codp.tile([P, 1024], U32, name="words", align_bytes=64)
-            scales[r] = codp.tile([P, 1024], U8, name="scales", align_bytes=64)
+            words[r] = codp.tile([P, 1024], U32, name="words", align_bytes=256)
+            scales[r] = codp.tile([P, 1024], U8, name="scales", align_bytes=256)
             for a, n in ((0, 2048), (2048, 1024)) if len(banks[r]) == 3 else ((0, 4096),):
                 nc.vector.quantize_mx(
                     out=words[r][:, a // 4 : (a + n) // 4].bitcast(FP8X4),
@@ -283,7 +283,7 @@ def tile_network_pa_kernel(
         def quantise_y1(sl):
             g, u = sl // 2, sl % 2
             if u == 0:
-                state[("y1", g)] = work.tile([P, BATCH, 4], BF16, name="y1_grouped", align_bytes=64)
+                state[("y1", g)] = work.tile([P, BATCH, 4], BF16, name="y1_grouped", align_bytes=256)
             t = state[("y1", g)]
             nc.vector.tensor_copy(out=t[:, :, 2 * u : 2 * u + 2], in_=state[("y", sl)][:].rearrange("p e c -> p c e"))
             if u == 1:

@@ -92,9 +92,9 @@ def tile_network_pa_kernel(
         zeros = const.tile([P, 512], BF16, name="zeros")
         nc.vector.memset(zeros[:], 0.0)
 
-        def fill(n):
+        def fill(n, spare=False):
             for i in range(n):
-                t = psum.tile([P, 2 * BATCH], F32, name="fill", tag="mx", bufs=2)
+                t = bank("fill") if spare else psum.tile([P, 2 * BATCH], F32, name="fill", tag="mx", bufs=2)
                 nc.tensor.matmul(out=t[:], lhsT=zeros[:, 0:P], rhs=zeros[:], start=True, stop=True)
 
         x_sb = load_rows(x, 512, "x_sb")
@@ -164,6 +164,8 @@ def tile_network_pa_kernel(
                             identity=ident[:],
                         )
                 banks[r].append(tp)
+                if r < 3 and len(banks[r]) == 1:
+                    fill(2)
             if r + RAW_BUFS < ROUNDS:
                 load_weights(r + RAW_BUFS)
 
@@ -373,8 +375,8 @@ def tile_network_pa_kernel(
                 rows.append((copy_rows(transpose_rows(h1_sb, 1), nc.vector.tensor_copy), 2))
             if todo:
                 transpose_weights(todo[0])
-            if s < 0:
-                fill(2)
+            if s == -2:
+                fill(1)
             if s == -2:
                 biases()
             if s in (11, 12):
@@ -416,4 +418,6 @@ def tile_network_pa_kernel(
             for values, a in rows:
                 quantise_rows(values, a)
             if 0 <= s < ROUNDS:
+                if s == CELL_ROUNDS:
+                    fill(2, True)
                 mx_passes(s, range(3, 4) if s == CELL_ROUNDS else None)

@@ -67,7 +67,7 @@ def tile_network_pa_kernel(
         state = {}
 
         def load_rows(ap, k, name):
-            t = const.tile([P, 2, k], BF16, name=name)
+            t = const.tile([P, 2, k], BF16, name=name, align_bytes=256)
             nc.sync.dma_start(out=t[:], in_=ap.rearrange("(h b) k -> b h k", h=2))
             return t
 
@@ -81,7 +81,7 @@ def tile_network_pa_kernel(
 
         ident = const.tile([P, P], F32, name="ident", align_bytes=256)
         make_identity(nc, ident[:])
-        bias_rows = const.tile([P, 256], BF16, name="bias_rows")
+        bias_rows = const.tile([P, 256], BF16, name="bias_rows", align_bytes=256)
         nc.vector.memset(bias_rows[:], 0.0)
         for v, bias in enumerate((bih1, bhh1, bih2, bhh2)):
             nc.scalar.dma_start(out=bias_rows[16 * v : 16 * v + 16, :], in_=bias.rearrange("(r w) -> r w", w=256))
@@ -89,7 +89,7 @@ def tile_network_pa_kernel(
         nc.vector.memset(warm[:], 0.0)
         nc.scalar.activation(out=warm[:], in_=warm[:], func=ACT.Sigmoid)
 
-        zeros = const.tile([P, 512], BF16, name="zeros")
+        zeros = const.tile([P, 512], BF16, name="zeros", align_bytes=256)
         nc.vector.memset(zeros[:], 0.0)
 
         def fill(n, spare=False):
@@ -221,7 +221,7 @@ def tile_network_pa_kernel(
 
         def apply_gate(r):
             cell, sl, gate = round_of(r)
-            t = work.tile([P, 2, BATCH], F32, name="gate%d" % gate)
+            t = work.tile([P, 2, BATCH], F32, name="gate%d" % gate, align_bytes=256)
             for e in range(2):
                 i = cell * 32 + gate * 8 + sl * 2 + e
                 nc.scalar.activation(
@@ -261,7 +261,7 @@ def tile_network_pa_kernel(
 
         def new_c(sl):
             ig = state[("ig", sl)]
-            t = work.tile([P, 2, BATCH], F32, name="new_c")
+            t = work.tile([P, 2, BATCH], F32, name="new_c", align_bytes=256)
             for part in parts(sl):
                 nc.vector.tensor_tensor(
                     out=t[:, part], in0=state[("fc", sl)][:, part], in1=ig[:, part], op=ALU.add
@@ -278,9 +278,19 @@ def tile_network_pa_kernel(
         def new_y(sl):
             if sl >= 4:
                 return
-            t = work.tile([P, 2, BATCH], F32, name="y")
+            t = work.tile([P, 2, BATCH], F32, name="y", align_bytes=256)
             nc.vector.tensor_tensor(out=t[:], in0=gates[(sl, 3)][:], in1=state[("tanh", sl)][:], op=ALU.mult)
             state[("y", sl)] = t
+
+        def last_y1():
+            t = state[("y1", 1)]
+            nc.vector.tensor_tensor(
+                out=t[:, :, 2:4],
+                in0=gates[(3, 3)][:].rearrange("p e c -> p c e"),
+                in1=state[("tanh", 3)][:].rearrange("p e c -> p c e"),
+                op=ALU.mult,
+            )
+            quantise_rows(t[:].rearrange("p c t -> p (c t)"), 6)
 
         def quantise_y1(sl):
             g, u = sl // 2, sl % 2
@@ -398,12 +408,14 @@ def tile_network_pa_kernel(
                 copy_weights(todo[0])
             if j == 2 and sl > 0:
                 new_c(sl)
+            if j == 3 and sl == 3:
+                last_y1()
             if j == 3:
                 new_y(sl)
-                if sl < 4:
+                if sl < 3:
                     quantise_y1(sl)
             if s == CELL_ROUNDS:
-                mx_passes(s, range(3))
+                mx_passes(s, range(2))
             for r in todo[1:]:
                 transpose_weights(r)
                 copy_weights(r)
@@ -418,6 +430,4 @@ def tile_network_pa_kernel(
             for values, a in rows:
                 quantise_rows(values, a)
             if 0 <= s < ROUNDS:
-                if s == CELL_ROUNDS:
-                    fill(2, True)
-                mx_passes(s, range(3, 4) if s == CELL_ROUNDS else None)
+                mx_passes(s, range(2, 4) if s == CELL_ROUNDS else None)

from contextlib import ExitStack

import concourse.mybir as mybir
from concourse.masks import make_identity

F32 = mybir.dt.float32
BF16 = mybir.dt.bfloat16
U32 = mybir.dt.uint32
U8 = mybir.dt.uint8
FP8X4 = mybir.dt.float8_e4m3fn_x4
ACT = mybir.ActivationFunctionType
ALU = mybir.AluOpType

P = 128
BATCH = 256
SLICE = 256
ROUNDS = 32
CELL_ROUNDS = 16
FLOPS = 2 * 256 * 4096 * (512 + 1024 + 1024 + 1024)

GATE_ORDER = (1, 0, 2, 3)
GATE_FUNC = (ACT.Sigmoid, ACT.Sigmoid, ACT.Tanh, ACT.Sigmoid)
RAW_BUFS = 9
AHEAD_1 = 2
AHEAD_2 = 3

K_PASSES = (
    ((0, 256, 0), (512, 512, 1), (768, 512, 2)),
    ((1024, 512, 3), (1280, 512, 4), (0, 512, 5), (256, 512, 6)),
)
ACT_PASSES = 7


def tile_network_pa_kernel(
    tc, x, h1, c1, h2, c2, Wih1, Whh1, bih1, bhh1, Wih2, Whh2, bih2, bhh2, out_0, out_1, out_2, out_3
):
    nc = tc.nc
    with ExitStack() as ctx:
        const = ctx.enter_context(tc.tile_pool(name="const", bufs=1))
        rawp = ctx.enter_context(tc.tile_pool(name="rawp", bufs=RAW_BUFS))
        grpp = ctx.enter_context(tc.tile_pool(name="grpp", bufs=4))
        codp = ctx.enter_context(tc.tile_pool(name="codp", bufs=AHEAD_2 + 2))
        work = ctx.enter_context(tc.tile_pool(name="work", bufs=2))
        psum = ctx.enter_context(tc.psum_pool(name="psum", bufs=2))
        ctx.enter_context(tc.manual_schedule())

        def by_round(w):
            return w.rearrange("(g v p e) k -> g v p (e k)", g=4, v=4, p=P, e=2)

        wih = (by_round(Wih1), by_round(Wih2))
        whh = (by_round(Whh1), by_round(Whh2))
        outs = [o.rearrange("(h b) l -> b h l", h=2) for o in (out_0, out_1, out_2, out_3)]

        def bank(name):
            return psum.tile([P, 512], F32, name=name, tag="tp", bufs=6)

        def round_of(r):
            return r // CELL_ROUNDS, (r % CELL_ROUNDS) // 4, GATE_ORDER[r % 4]

        raw = {}
        banks = {}
        grouped = {}
        words = {}
        scales = {}
        sums = {}
        gates = {}
        state = {}

        def load_rows(ap, k, name):
            t = const.tile([P, 2, k], BF16, name=name, align_bytes=256)
            nc.sync.dma_start(out=t[:], in_=ap.rearrange("(h b) k -> b h k", h=2))
            return t

        def load_weights(r):
            cell, sl, gate = round_of(r)
            t = rawp.tile([P, 4096], BF16, name="raw", align_bytes=256)
            n_ih = 1024 if cell == 0 else 2048
            nc.sync.dma_start(out=t[:, 0:n_ih], in_=wih[cell][gate, sl])
            nc.sync.dma_start(out=t[:, n_ih : n_ih + 2048], in_=whh[cell][gate, sl])
            raw[r] = t

        ident = const.tile([P, P], F32, name="ident", align_bytes=256)
        make_identity(nc, ident[:])
        bias_rows = const.tile([P, 256], BF16, name="bias_rows", align_bytes=256)
        nc.vector.memset(bias_rows[:], 0.0)
        for v, bias in enumerate((bih1, bhh1, bih2, bhh2)):
            nc.scalar.dma_start(out=bias_rows[16 * v : 16 * v + 16, :], in_=bias.rearrange("(r w) -> r w", w=256))
        warm = const.tile([P, 1], F32, name="warm")
        nc.vector.memset(warm[:], 0.0)
        nc.scalar.activation(out=warm[:], in_=warm[:], func=ACT.Sigmoid)

        zeros = const.tile([P, 512], BF16, name="zeros", align_bytes=256)
        nc.vector.memset(zeros[:], 0.0)

        def fill(n, spare=False):
            for i in range(n):
                t = bank("fill") if spare else psum.tile([P, 2 * BATCH], F32, name="fill", tag="mx", bufs=2)
                nc.tensor.matmul(out=t[:], lhsT=zeros[:, 0:P], rhs=zeros[:], start=True, stop=True)

        x_sb = load_rows(x, 512, "x_sb")
        load_weights(0)
        h1_sb = load_rows(h1, 1024, "h1_sb")
        for r in range(1, 4):
            load_weights(r)
        for r in range(4, 6):
            load_weights(r)
        c1_sb = load_rows(c1, 1024, "c1_sb")
        for r in range(6, RAW_BUFS):
            load_weights(r)
        c_sb = [c1_sb, None]

        act_words = const.tile([P, ACT_PASSES, BATCH], U32, name="act_words", align_bytes=256)
        act_scales = const.tile([P, ACT_PASSES, BATCH], U8, name="act_scales", align_bytes=256)
        bias_f32 = const.tile([P, P], F32, name="bias_f32")
        bias_sum = const.tile([P, 64], F32, name="bias_sum")

        def transpose_rows(src, g):
            src_words = src[:].bitcast(F32)
            tp = bank("tpa")
            for u in range(2):
                for h in range(2):
                    nc.tensor.transpose(
                        out=tp[:, (u * 2 + h) * P : (u * 2 + h + 1) * P],
                        in_=src_words[:, h, g * 256 + u * P : g * 256 + (u + 1) * P],
                        identity=ident[:],
                    )
            return tp

        def copy_rows(tp, copier):
            t = work.tile([P, 4 * BATCH], BF16, name="act_grouped", align_bytes=256)
            copier(
                out=t[:].bitcast(F32).rearrange("p (c u) -> p c u", u=2), in_=tp[:].rearrange("p (u c) -> p c u", u=2)
            )
            return t[:]

        def quantise_rows(values, a):
            nc.vector.quantize_mx(
                out=act_words[:, a, :].bitcast(FP8X4), scales=act_scales[:, a, :], in_=values
            )

        def biases():
            tp = bank("tpb")
            nc.tensor.transpose(out=tp[:, 0:P], in_=bias_rows[:].bitcast(F32), identity=ident[:])
            nc.vector.tensor_copy(out=bias_f32[:], in_=tp[:, 0:64].bitcast(BF16))
            for cell in range(2):
                nc.vector.tensor_tensor(
                    out=bias_sum[:, cell * 32 : cell * 32 + 32],
                    in0=bias_f32[:, cell * 64 : cell * 64 + 32],
                    in1=bias_f32[:, cell * 64 + 32 : cell * 64 + 64],
                    op=ALU.add,
                )

        def transpose_weights(r):
            raw_words = raw[r][:].bitcast(F32)
            banks[r] = []
            for first, e_step, a in K_PASSES[round_of(r)[0]]:
                tp = bank("tpw")
                for e in range(2):
                    for u in range(2):
                        w = first + e * e_step + u * P
                        nc.tensor.transpose(
                            out=tp[:, (e * 2 + u) * P : (e * 2 + u + 1) * P],
                            in_=raw_words[:, w : w + P],
                            identity=ident[:],
                        )
                banks[r].append(tp)
                if r < 3 and len(banks[r]) == 1:
                    fill(2)
            if r + RAW_BUFS < ROUNDS:
                load_weights(r + RAW_BUFS)

        def copy_weights(r):
            grouped[r] = grpp.tile([P, 4096], BF16, name="grouped", align_bytes=256)
            n = len(banks[r])
            for kp in range(n):
                copier = nc.vector.tensor_copy if kp == n - 1 and (r >= 16 or r % 2 != 1) else nc.scalar.copy
                copier(
                    out=grouped[r][:, kp * 1024 : (kp + 1) * 1024]
                    .bitcast(F32)
                    .rearrange("p (e n u) -> p e n u", e=2, u=2),
                    in_=banks[r][kp][:].rearrange("p (e u n) -> p e n u", e=2, u=2),
                )

        def quantise_weights(r):
            words[r] = codp.tile([P, 1024], U32, name="words", align_bytes=256)
            scales[r] = codp.tile([P, 1024], U8, name="scales", align_bytes=256)
            for a, n in ((0, 2048), (2048, 1024)) if len(banks[r]) == 3 else ((0, 4096),):
                nc.vector.quantize_mx(
                    out=words[r][:, a // 4 : (a + n) // 4].bitcast(FP8X4),
                    scales=scales[r][:, a // 4 : (a + n) // 4],
                    in_=grouped[r][:, a : a + n],
                )

        def mx_passes(r, kps=None):
            passes = K_PASSES[round_of(r)[0]]
            if kps is None or 0 in kps:
                if r >= 30:
                    sums[r] = [bank("sums"), bank("sums")]
                else:
                    sums[r] = [psum.tile([P, 2 * BATCH], F32, name="sums", tag="mx", bufs=2)]
                    if kps is not None:
                        sums[r].append(psum.tile([P, 2 * BATCH], F32, name="sums", tag="mx", bufs=2))
            for e in range(2):
                for kp in kps or range(len(passes)):
                    a = passes[kp][2]
                    c0 = kp * 256 + e * P
                    nc.tensor.matmul_mx(
                        out=sum_of(r, e),
                        lhsT=words[r][:, c0 : c0 + P].bitcast(FP8X4),
                        lhsT_scale=scales[r][:, c0 : c0 + P],
                        rhs=act_words[:, a, :].bitcast(FP8X4),
                        rhs_scale=act_scales[:, a, :],
                        start=(kp == 0),
                        stop=(kp == len(passes) - 1),
                    )

        def sum_of(r, e):
            if len(sums[r]) == 2:
                return sums[r][e][:, 0:BATCH]
            return sums[r][0][:, e * BATCH : (e + 1) * BATCH]

        def apply_gate(r):
            cell, sl, gate = round_of(r)
            t = work.tile([P, 2, BATCH], F32, name="gate%d" % gate, align_bytes=256)
            for e in range(2):
                i = cell * 32 + gate * 8 + sl * 2 + e
                nc.scalar.activation(
                    out=t[:, e, :],
                    in_=sum_of(r, e),
                    func=GATE_FUNC[gate],
                    bias=bias_sum[:, i : i + 1],
                )
            gates[(r // 4, gate)] = t

        def transpose_c(sl):
            c_words = c_sb[sl // 4][:].bitcast(F32)
            tp = bank("tpc")
            for h in range(2):
                nc.tensor.transpose(
                    out=tp[:, h * P : (h + 1) * P],
                    in_=c_words[:, h, (sl % 4) * P : (sl % 4 + 1) * P],
                    identity=ident[:],
                )
            state[("c", sl)] = tp[:, 0:BATCH].bitcast(BF16).rearrange("p (c e) -> p e c", e=2)

        def forget(sl):
            t = work.tile([P, 2, BATCH], F32, name="fc")
            nc.vector.tensor_tensor(out=t[:], in0=gates[(sl, 1)][:], in1=state[("c", sl)], op=ALU.mult)
            state[("fc", sl)] = t

        def parts(sl):
            return (slice(0, 1), slice(1, 2)) if sl == 7 else (slice(0, 2),)

        def input_part(sl):
            ig = work.tile([P, 2, BATCH], F32, name="ig")
            for part in parts(sl):
                nc.vector.tensor_tensor(
                    out=ig[:, part], in0=gates[(sl, 0)][:, part], in1=gates[(sl, 2)][:, part], op=ALU.mult
                )
            state[("ig", sl)] = ig

        def new_c(sl):
            ig = state[("ig", sl)]
            t = work.tile([P, 2, BATCH], F32, name="new_c", align_bytes=256)
            for part in parts(sl):
                nc.vector.tensor_tensor(
                    out=t[:, part], in0=state[("fc", sl)][:, part], in1=ig[:, part], op=ALU.add
                )
            state[("nc", sl)] = t

        def tanh_c(sl):
            if sl >= 4:
                return
            t = work.tile([P, 2, BATCH], F32, name="tanh")
            nc.scalar.activation(out=t[:], in_=state[("nc", sl)][:], func=ACT.Tanh)
            state[("tanh", sl)] = t

        def new_y(sl):
            if sl >= 4:
                return
            t = work.tile([P, 2, BATCH], F32, name="y", align_bytes=256)
            nc.vector.tensor_tensor(out=t[:], in0=gates[(sl, 3)][:], in1=state[("tanh", sl)][:], op=ALU.mult)
            state[("y", sl)] = t

        def last_y1():
            t = state[("y1", 1)]
            nc.vector.tensor_tensor(
                out=t[:, :, 2:4],
                in0=gates[(3, 3)][:].rearrange("p e c -> p c e"),
                in1=state[("tanh", 3)][:].rearrange("p e c -> p c e"),
                op=ALU.mult,
            )
            quantise_rows(t[:].rearrange("p c t -> p (c t)"), 6)

        def quantise_y1(sl):
            g, u = sl // 2, sl % 2
            if u == 0:
                state[("y1", g)] = work.tile([P, BATCH, 4], BF16, name="y1_grouped", align_bytes=256)
            t = state[("y1", g)]
            nc.vector.tensor_copy(out=t[:, :, 2 * u : 2 * u + 2], in_=state[("y", sl)][:].rearrange("p e c -> p c e"))
            if u == 1:
                quantise_rows(t[:].rearrange("p c t -> p (c t)"), 5 + g)

        def transpose_result(kind, sl):
            src = gates[(sl, 3)] if (kind == "y" and sl >= 4) else state[(kind, sl)]
            for part in batch_parts(sl):
                tp = bank("tpo")
                for h in part:
                    for e in range(2):
                        nc.tensor.transpose(
                            out=tp[:, (h * 2 + e) * P : (h * 2 + e + 1) * P],
                            in_=src[:, e, h * P : (h + 1) * P],
                            identity=ident[:],
                        )
                state[("T" + kind, sl, part[0])] = tp

        def batch_parts(sl):
            return ((0,), (1,)) if sl == 7 else ((0, 1),)

        def store_result(kind, sl):
            u = sl % 2
            if u == 0:
                state["out" + kind] = work.tile([P, 2, 2 * SLICE], F32, name="out" + kind)
            t = state["out" + kind]
            out = outs[(sl // 4) * 2 + (0 if kind == "y" else 1)]
            c0 = (sl % 4 - u) * SLICE
            if kind == "nc" and sl >= 4:
                state[("tanh_t", sl)] = work.tile([P, 512], F32, name="tanh_t")
            for part in batch_parts(sl):
                hs = slice(part[0], part[-1] + 1)
                cols = slice(part[0] * 256, (part[-1] + 1) * 256)
                tp = state[("T" + kind, sl, part[0])][:, cols]
                n = len(part)
                out_view = t[:, hs, u * SLICE : (u + 1) * SLICE].rearrange("b h (p e) -> b h p e", e=2)
                in_view = tp.rearrange("b (h e p) -> b h p e", h=n, e=2)
                if sl < 4:
                    copier = nc.scalar.copy if kind == "y" else nc.vector.tensor_copy
                    copier(out=out_view, in_=in_view)
                elif kind == "nc":
                    nc.scalar.activation(out=state[("tanh_t", sl)][:, cols], in_=tp, func=ACT.Tanh)
                    nc.vector.tensor_copy(out=out_view, in_=in_view)
                else:
                    nc.vector.tensor_tensor(
                        out=out_view,
                        in0=in_view,
                        in1=state[("tanh_t", sl)][:, cols].rearrange("b (h e p) -> b h p e", h=n, e=2),
                        op=ALU.mult,
                    )
                if sl >= 6:
                    nc.sync.dma_start(
                        out=out[:, hs, c0 + u * SLICE : c0 + (u + 1) * SLICE], in_=t[:, hs, u * SLICE : (u + 1) * SLICE]
                    )
            if sl < 6 and u == 1:
                nc.sync.dma_start(out=out[:, :, c0 : c0 + 2 * SLICE], in_=t[:])

        fill(6)
        def rounds_to_transpose(s):
            if s < CELL_ROUNDS:
                return [s + AHEAD_1]
            if s == CELL_ROUNDS:
                return list(range(s + AHEAD_1, s + AHEAD_2 + 1))
            return [s + AHEAD_2] if s + AHEAD_2 < ROUNDS else []

        due = {}
        for sl in range(8):
            wait = 2 if sl < 7 else 1
            due[4 * sl + 3 + wait] = ("nc", sl)
            due[4 * sl + 4 + wait] = ("y", sl)

        for s in range(-AHEAD_1, ROUNDS + 2):
            if s == 3:
                h2_sb = load_rows(h2, 1024, "h2_sb")
            if s == 10:
                c_sb[1] = load_rows(c2, 1024, "c2_sb")
            todo = rounds_to_transpose(s)
            gated = s - 1
            has_gate = 0 <= gated < ROUNDS
            j = gated % 4 if has_gate else -1
            sl = gated // 4
            rows = []
            if s == -2:
                rows.append((copy_rows(transpose_rows(x_sb, 0), nc.scalar.copy), 0))
            if s == -1:
                rows.append((copy_rows(transpose_rows(h1_sb, 0), nc.scalar.copy), 1))
                rows.append((copy_rows(transpose_rows(h1_sb, 1), nc.vector.tensor_copy), 2))
            if todo:
                transpose_weights(todo[0])
            if s == -2:
                fill(1)
            if s == -2:
                biases()
            if s in (11, 12):
                h2_bank = transpose_rows(h2_sb, s - 11)
            if (j == 2 if sl == 0 else j == 1):
                transpose_c(sl)
            if s in due:
                transpose_result(due[s][0], due[s][1])
            if has_gate:
                apply_gate(gated)
            if j == 3:
                tanh_c(sl)
            if s > -AHEAD_1:
                for r in rounds_to_transpose(s - 1):
                    quantise_weights(r)
            if j == 2:
                input_part(sl)
            if todo:
                copy_weights(todo[0])
            if j == 2 and sl > 0:
                new_c(sl)
            if j == 3 and sl == 3:
                last_y1()
            if j == 3:
                new_y(sl)
                if sl < 3:
                    quantise_y1(sl)
            if s == CELL_ROUNDS:
                mx_passes(s, range(2))
            for r in todo[1:]:
                transpose_weights(r)
                copy_weights(r)
            if s in due:
                store_result(due[s][0], due[s][1])
            if (j == 2 if sl == 0 else j == 1):
                forget(sl)
            if j == 2 and sl == 0:
                new_c(sl)
            if s in (11, 12):
                rows.append((copy_rows(h2_bank, nc.scalar.copy), 3 + s - 11))
            for values, a in rows:
                quantise_rows(values, a)
            if 0 <= s < ROUNDS:
                mx_passes(s, range(2, 4) if s == CELL_ROUNDS else None)
